import numpy as np
import ml_dtypes


def mxq(x, axis, fmt="e4m3"):
    dtype, down = {"e4m3": (ml_dtypes.float8_e4m3fn, 7), "e5m2": (ml_dtypes.float8_e5m2, 14)}[fmt]
    v = np.moveaxis(np.asarray(x, np.float32).astype(ml_dtypes.bfloat16).astype(np.float64), axis, -1)
    blocks = v.reshape(v.shape[:-1] + (-1, 32))
    amax = np.abs(blocks).max(-1, keepdims=True)
    byte = np.maximum(np.where(amax > 0, np.frexp(amax)[1] - 1 + 127, 0) - down, 1)
    scale = np.exp2(byte - 127.0)
    codes = (blocks / scale).astype(np.float32).astype(dtype).astype(np.float64)
    return np.moveaxis((codes * scale).reshape(v.shape), -1, axis)


WIDE = False


def mx_kscale(k):
    if not WIDE:
        return np.ones(k)
    levels = np.array([10, -10, 5, -5, 0])
    a = np.random.permutation(np.resize(levels, k // 512 * 4)).reshape(k // 512, 4)
    idx = np.arange(k)
    return np.exp2(a[idx // 512, idx % 128 // 32])


BF16 = ml_dtypes.bfloat16


def bf(x):
    return np.asarray(x, np.float32).astype(BF16)


def f64(x):
    return np.asarray(x).astype(np.float64)


B, N, E, F, H, K, C, G, DEG = 8, 2048, 512, 32, 64, 8, 32, 64, 32


def incidence(rows, cols):
    return (np.random.uniform(size=(rows, cols)) < DEG / N) * np.random.uniform(0.5, 1.5, (rows, cols))


def setup_inputs():
    s, t = mx_kscale(N), mx_kscale(E)
    return {"x": bf(np.random.standard_normal((B, N, C)) / s[None, :, None]),
            "rinc": bf(incidence(E, N) * s[None, :]),
            "linc": bf(incidence(N, E) * t[None, :]),
            "edge_w": bf(np.random.standard_normal((E, K)) * 0.25 / t[:, None])}


def reference(x, rinc, linc, edge_w):
    z = mxq(f64(rinc), 1, "e4m3") @ mxq(f64(x), 1, "e4m3")
    m = (z[:, :, :, None] * f64(edge_w)[None, :, None, :]).reshape(B, E, C * K)
    return mxq(f64(linc), 1, "e4m3") @ mxq(m, 1, "e4m3")

@@ -1,0 +1,153 @@
+from contextlib import ExitStack
+
+import concourse.mybir as mybir
+from concourse.masks import make_identity
+
+FP8X4 = mybir.dt.float8_e4m3fn_x4
+BF16 = mybir.dt.bfloat16
+F32 = mybir.dt.float32
+U32 = mybir.dt.uint32
+U8 = mybir.dt.uint8
+
+P = 128
+B, NODES, EDGES, C, KW = 8, 2048, 512, 32, 8
+W = C * KW
+G = NODES // 512
+J = NODES // P
+FLOPS = 2 * EDGES * NODES * B * C + 2 * NODES * EDGES * B * W
+
+VEC_BANKS = (1, 4, 6)
+
+
+def tile_sgcn_pa_t_kernel(tc, x, rinc, linc, edge_w, out):
+    nc = tc.nc
+    with ExitStack() as ctx:
+        keep = ctx.enter_context(tc.tile_pool(name="keep", bufs=1))
+        stage = ctx.enter_context(tc.tile_pool(name="stage", bufs=6))
+        ps_t = ctx.enter_context(tc.psum_pool(name="ps_t", bufs=2))
+        ps_z = ctx.enter_context(tc.psum_pool(name="ps_z", bufs=1))
+        ps_o = ctx.enter_context(tc.psum_pool(name="ps_o", bufs=4))
+
+        ident = keep.tile([P, P], F32, name="ident")
+        make_identity(nc, ident[:])
+
+        ew_raw = keep.tile([P, 2, 2 * KW], BF16, name="ew_raw")
+        nc.scalar.dma_start(out=ew_raw[:], in_=edge_w.rearrange("(u p e) k -> p u (e k)", u=2, p=P, e=2))
+        xs = []
+        for g in range(G):
+            t = keep.tile([P, B, 4 * C], BF16, name="xs%d" % g)
+            nc.sync.dma_start(out=t[:], in_=x[:, 512 * g:512 * (g + 1), :].rearrange("b (p t) c -> p b (t c)", t=4))
+            xs.append(t)
+        rs = []
+        r_view = rinc.rearrange("(u p e) n -> u e p n", u=2, p=P, e=2)
+        for te in range(4):
+            t = keep.tile([P, NODES], BF16, name="rs%d" % te)
+            nc.sync.dma_start(out=t[:], in_=r_view[te // 2, te % 2])
+            rs.append(t)
+        ls = []
+        l_view = linc.rearrange("(p j) e -> p j e", j=J)
+        for q in range(4):
+            t = keep.tile([P, 4, EDGES], BF16, name="ls%d" % q)
+            nc.sync.dma_start(out=t[:], in_=l_view[:, 4 * q:4 * q + 4, :])
+            ls.append(t)
+
+        ewf = keep.tile([P, KW, 4], F32, name="ewf")
+        nc.vector.tensor_copy(
+            out=ewf[:].rearrange("p k (u e) -> p k u e", u=2),
+            in_=ew_raw[:].rearrange("p u (e k) -> p k u e", e=2),
+        )
+
+        x_codes, x_scales = [], []
+        for g in range(G):
+            xg = keep.tile([P, B * C * 4], BF16, name="xg%d" % g, align_bytes=64)
+            nc.vector.tensor_copy(
+                out=xg[:].rearrange("p (b c t) -> p b c t", b=B, c=C),
+                in_=xs[g][:].rearrange("p b (t c) -> p b c t", t=4),
+            )
+            cd = keep.tile([P, B * C], U32, name="xc%d" % g, align_bytes=64)
+            sc = keep.tile([P, B * C], U8, name="xsc%d" % g, align_bytes=64)
+            nc.vector.quantize_mx(out=cd[:].bitcast(FP8X4), scales=sc[:], in_=xg[:])
+            x_codes.append(cd)
+            x_scales.append(sc)
+
+        z = [ps_z.tile([P, 4, P], F32, name="z%d" % h) for h in range(2)]
+        for te in range(4):
+            rw = rs[te][:].bitcast(F32)
+            rg = keep.tile([P, G * P * 4], BF16, name="rg%d" % te, align_bytes=64)
+            rgw = rg[:].bitcast(F32).rearrange("p (g e h) -> p g e h", g=G, h=2)
+            for gp in range(2):
+                tp = ps_t.tile([P, 2, 2, P], F32, name="tp")
+                for gg in range(2):
+                    g = 2 * gp + gg
+                    for h in range(2):
+                        nc.tensor.transpose(tp[:, gg, h, :], rw[:, 256 * g + h:256 * (g + 1):2], ident[:])
+                src = tp[:].rearrange("p g h e -> p g e h")
+                if gp == 0:
+                    nc.vector.tensor_copy(out=rgw[:, 0:2], in_=src)
+                else:
+                    nc.scalar.copy(out=rgw[:, 2:4], in_=src)
+            cd = keep.tile([P, G * P], U32, name="rc%d" % te, align_bytes=64)
+            sc = keep.tile([P, G * P], U8, name="rsc%d" % te, align_bytes=64)
+            nc.vector.quantize_mx(out=cd[:].bitcast(FP8X4), scales=sc[:], in_=rg[:])
+            for h in range(2):
+                for g in range(G):
+                    nc.tensor.matmul_mx(
+                        out=z[h][:, te, :],
+                        lhsT=cd[:, P * g:P * (g + 1)].bitcast(FP8X4),
+                        lhsT_scale=sc[:, P * g:P * (g + 1)],
+                        rhs=x_codes[g][:, P * h:P * (h + 1)].bitcast(FP8X4),
+                        rhs_scale=x_scales[g][:, P * h:P * (h + 1)],
+                        start=(g == 0),
+                        stop=(g == G - 1),
+                    )
+
+        l_codes, l_scales = [], []
+        for q in range(4):
+            lw = ls[q][:].bitcast(F32)
+            lg = keep.tile([P, 4 * P * 4], BF16, name="lg%d" % q, align_bytes=64)
+            lgw = lg[:].bitcast(F32).rearrange("p (j n u) -> p j n u", j=4, u=2)
+            for jp in range(2):
+                tp = ps_t.tile([P, 2, 2, P], F32, name="tp")
+                for jj in range(2):
+                    for u in range(2):
+                        nc.tensor.transpose(tp[:, jj, u, :], lw[:, 2 * jp + jj, P * u:P * (u + 1)], ident[:])
+                nc.scalar.copy(out=lgw[:, 2 * jp:2 * jp + 2], in_=tp[:].rearrange("p j u n -> p j n u"))
+            cd = keep.tile([P, 4 * P], U32, name="lc%d" % q, align_bytes=64)
+            sc = keep.tile([P, 4 * P], U8, name="lsc%d" % q, align_bytes=64)
+            nc.vector.quantize_mx(out=cd[:].bitcast(FP8X4), scales=sc[:], in_=lg[:])
+            l_codes.append(cd)
+            l_scales.append(sc)
+
+        o_view = out.rearrange("b (p j) w -> b p j w", j=J)
+        for b in range(B):
+            mg = keep.tile([P, W * 4], BF16, name="mg%d" % b, align_bytes=64)
+            nc.vector.tensor_tensor(
+                out=mg[:].rearrange("p (c k t) -> p c k t", c=C, k=KW),
+                in0=z[b // 4][:, :, C * (b % 4):C * (b % 4 + 1)].rearrange("p t c -> p c t").unsqueeze(2).to_broadcast([P, C, KW, 4]),
+                in1=ewf[:].unsqueeze(1).to_broadcast([P, C, KW, 4]),
+                op=mybir.AluOpType.mult,
+            )
+            mc = keep.tile([P, W], U32, name="mc%d" % b, align_bytes=64)
+            ms = keep.tile([P, W], U8, name="msc%d" % b, align_bytes=64)
+            nc.vector.quantize_mx(out=mc[:].bitcast(FP8X4), scales=ms[:], in_=mg[:])
+            for half in range(2):
+                st = stage.tile([P, 8, W], F32, name="st")
+                for jq in range(4):
+                    jp = 4 * half + jq
+                    o = ps_o.tile([P, 2, W], F32, name="o")
+                    for jj in range(2):
+                        j = 2 * jp + jj
+                        nc.tensor.matmul_mx(
+                            out=o[:, jj, :],
+                            lhsT=l_codes[j // 4][:, P * (j % 4):P * (j % 4 + 1)].bitcast(FP8X4),
+                            lhsT_scale=l_scales[j // 4][:, P * (j % 4):P * (j % 4 + 1)],
+                            rhs=mc[:].bitcast(FP8X4),
+                            rhs_scale=ms[:],
+                            start=True,
+                            stop=True,
+                        )
+                    if jp in VEC_BANKS:
+                        nc.vector.tensor_copy(out=st[:, 2 * jq:2 * jq + 2, :], in_=o[:])
+                    else:
+                        nc.scalar.copy(out=st[:, 2 * jq:2 * jq + 2, :], in_=o[:])
+                nc.sync.dma_start(out=o_view[b, :, 8 * half:8 * half + 8, :], in_=st[:])

@@ -12,44 +12,88 @@ U8 = mybir.dt.uint8
 P = 128
 B, NODES, EDGES, C, KW = 8, 2048, 512, 32, 8
 W = C * KW
-G = NODES // 512
 J = NODES // P
 FLOPS = 2 * EDGES * NODES * B * C + 2 * NODES * EDGES * B * W
 
-VEC_BANKS = (1, 4, 6)
+STORES = ((1, 1, 2, 2, 2), (2, 2, 4), (4, 4), (4, 4), (4, 4), (4, 4), (4, 4), (4, 4))
+ST_BUFS = {1: 2, 2: 5, 4: 8}
+
+ORDER = (
+    ("xr", 0), ("tr", 0, 0), ("xq", 0), ("cr", 0, 0, "S"), ("tr", 0, 1), ("cr", 0, 1, "V"),
+    ("tr", 1, 0), ("rq", 0, 0), ("cr", 1, 0, "S"), ("tr", 1, 1), ("rq", 0, 1), ("tr", 2, 0),
+    ("rq", 1, 0), ("cr", 1, 1, "S"), ("tr", 2, 1), ("rq", 1, 1), ("cr", 2, 0, "S"), ("cr", 2, 1, "V"),
+    ("tr", 3, 0), ("tr", 3, 1), ("rq", 2, 0), ("cr", 3, 0, "S"), ("rq", 2, 1), ("cr", 3, 1, "S"),
+    ("z", 0, 0, 0), ("rq", 3, 0), ("z", 0, 0, 1), ("z", 1, 0, 0), ("rq", 3, 1), ("z", 1, 0, 1),
+    ("z", 2, 0, 0), ("z", 2, 0, 1), ("z", 3, 0, 0), ("z", 3, 0, 1), ("tl", 0, 0), ("m", 0),
+    ("cl", 0, 0, "S"), ("tl", 0, 1), ("tl", 1, 0), ("tl", 1, 1), ("lq", 0, 0), ("cl", 0, 1, "S"),
+    ("mq", 0), ("tl", 2, 0), ("cl", 1, 0, "S"), ("lq", 0, 1), ("tl", 2, 1), ("o", 0, 0),
+    ("cl", 1, 1, "V"), ("cl", 2, 0, "S"), ("o", 0, 1), ("co", 0, 0, "V"), ("st", 0, 0), ("co", 0, 1, "S"),
+    ("st", 0, 1), ("tl", 3, 0), ("lq", 1, 0), ("tl", 3, 1), ("cl", 2, 1, "S"), ("lq", 1, 1),
+    ("lq", 2, 0), ("o", 0, 2), ("cl", 3, 0, "S"), ("lq", 2, 1), ("o", 0, 3), ("co", 0, 2, "S"),
+    ("m", 1), ("o", 0, 4), ("o", 0, 5), ("co", 0, 3, "S"), ("st", 0, 2), ("lq", 3, 0),
+    ("cl", 3, 1, "S"), ("co", 0, 4, "V"), ("co", 0, 5, "S"), ("st", 0, 4), ("o", 0, 6), ("lq", 3, 1),
+    ("mq", 1), ("co", 0, 6, "S"), ("o", 0, 7), ("m", 2), ("co", 0, 7, "S"), ("st", 0, 6),
+    ("o", 1, 0), ("o", 1, 1), ("co", 1, 0, "S"), ("o", 1, 2), ("co", 1, 1, "V"), ("st", 1, 0),
+    ("o", 1, 3), ("co", 1, 2, "S"), ("o", 1, 4), ("co", 1, 3, "V"), ("st", 1, 2), ("o", 1, 5),
+    ("o", 1, 6), ("co", 1, 4, "S"), ("mq", 2), ("o", 1, 7), ("co", 1, 5, "V"), ("co", 1, 6, "S"),
+    ("o", 2, 0), ("co", 1, 7, "S"), ("st", 1, 4), ("co", 2, 0, "V"), ("o", 2, 1), ("o", 2, 2),
+    ("co", 2, 1, "S"), ("o", 2, 3), ("co", 2, 2, "V"), ("o", 2, 4), ("co", 2, 3, "S"), ("st", 2, 0),
+    ("o", 2, 5), ("m", 3), ("o", 2, 6), ("co", 2, 4, "S"), ("o", 2, 7), ("co", 2, 5, "S"),
+    ("mq", 3), ("co", 2, 6, "S"), ("co", 2, 7, "V"), ("st", 2, 4), ("o", 3, 0), ("co", 3, 0, "S"),
+    ("xr", 1), ("o", 3, 1), ("o", 3, 2), ("co", 3, 1, "S"), ("o", 3, 3), ("o", 3, 4),
+    ("o", 3, 5), ("xq", 1), ("co", 3, 2, "S"), ("o", 3, 6), ("o", 3, 7), ("co", 3, 3, "S"),
+    ("st", 3, 0), ("co", 3, 4, "V"), ("z", 0, 1, 0), ("co", 3, 5, "S"), ("z", 0, 1, 1), ("co", 3, 6, "V"),
+    ("z", 1, 1, 0), ("z", 1, 1, 1), ("co", 3, 7, "S"), ("st", 3, 4), ("z", 2, 1, 0), ("z", 2, 1, 1),
+    ("z", 3, 1, 0), ("z", 3, 1, 1), ("m", 4), ("mq", 4), ("m", 5), ("o", 4, 0),
+    ("co", 4, 0, "S"), ("o", 4, 1), ("o", 4, 2), ("co", 4, 1, "V"), ("co", 4, 2, "S"), ("o", 4, 3),
+    ("o", 4, 4), ("co", 4, 3, "V"), ("st", 4, 0), ("o", 4, 5), ("co", 4, 4, "S"), ("o", 4, 6),
+    ("mq", 5), ("o", 4, 7), ("co", 4, 5, "S"), ("co", 4, 6, "V"), ("co", 4, 7, "S"), ("st", 4, 4),
+    ("o", 5, 0), ("co", 5, 0, "V"), ("o", 5, 1), ("co", 5, 1, "S"), ("o", 5, 2), ("o", 5, 3),
+    ("co", 5, 2, "V"), ("co", 5, 3, "S"), ("st", 5, 0), ("o", 5, 4), ("o", 5, 5), ("m", 6),
+    ("o", 5, 6), ("co", 5, 4, "S"), ("o", 5, 7), ("co", 5, 5, "S"), ("mq", 6), ("co", 5, 6, "S"),
+    ("co", 5, 7, "V"), ("st", 5, 4), ("o", 6, 0), ("co", 6, 0, "S"), ("o", 6, 1), ("m", 7),
+    ("o", 6, 2), ("co", 6, 1, "S"), ("o", 6, 3), ("o", 6, 4), ("co", 6, 2, "V"), ("o", 6, 5),
+    ("co", 6, 3, "S"), ("st", 6, 0), ("o", 6, 6), ("mq", 7), ("o", 6, 7), ("co", 6, 4, "S"),
+    ("co", 6, 5, "V"), ("co", 6, 6, "S"), ("o", 7, 0), ("co", 6, 7, "V"), ("st", 6, 4), ("o", 7, 1),
+    ("co", 7, 0, "S"), ("o", 7, 2), ("co", 7, 1, "V"), ("o", 7, 3), ("co", 7, 2, "S"), ("o", 7, 4),
+    ("co", 7, 3, "V"), ("st", 7, 0), ("o", 7, 5), ("co", 7, 4, "S"), ("o", 7, 6), ("o", 7, 7),
+    ("co", 7, 5, "V"), ("co", 7, 6, "S"), ("co", 7, 7, "V"), ("st", 7, 4),
+)
 
 
 def tile_sgcn_pa_t_kernel(tc, x, rinc, linc, edge_w, out):
     nc = tc.nc
     with ExitStack() as ctx:
         keep = ctx.enter_context(tc.tile_pool(name="keep", bufs=1))
-        stage = ctx.enter_context(tc.tile_pool(name="stage", bufs=6))
-        ps_t = ctx.enter_context(tc.psum_pool(name="ps_t", bufs=2))
+        stage = ctx.enter_context(tc.tile_pool(name="stage", bufs=1))
         ps_z = ctx.enter_context(tc.psum_pool(name="ps_z", bufs=1))
-        ps_o = ctx.enter_context(tc.psum_pool(name="ps_o", bufs=4))
+        ps = ctx.enter_context(tc.psum_pool(name="ps", bufs=6))
+        ctx.enter_context(tc.manual_schedule())
 
         ident = keep.tile([P, P], F32, name="ident")
         make_identity(nc, ident[:])
 
         ew_raw = keep.tile([P, 2, 2 * KW], BF16, name="ew_raw")
         nc.scalar.dma_start(out=ew_raw[:], in_=edge_w.rearrange("(u p e) k -> p u (e k)", u=2, p=P, e=2))
-        xs = []
-        for g in range(G):
-            t = keep.tile([P, B, 4 * C], BF16, name="xs%d" % g)
-            nc.sync.dma_start(out=t[:], in_=x[:, 512 * g:512 * (g + 1), :].rearrange("b (p t) c -> p b (t c)", t=4))
-            xs.append(t)
-        rs = []
+
+        xs = [keep.tile([P, 4, 4, 4 * C], BF16, name="xs%d" % h) for h in range(2)]
+        rs_whole = [keep.tile([P, NODES], BF16, name="rs%d" % te) for te in range(3)]
+        rs_last = [keep.tile([P, NODES // 2], BF16, name="rs3_%d" % k) for k in range(2)]
+        ls = [keep.tile([P, 4, EDGES], BF16, name="ls%d" % q) for q in range(4)]
         r_view = rinc.rearrange("(u p e) n -> u e p n", u=2, p=P, e=2)
-        for te in range(4):
-            t = keep.tile([P, NODES], BF16, name="rs%d" % te)
-            nc.sync.dma_start(out=t[:], in_=r_view[te // 2, te % 2])
-            rs.append(t)
-        ls = []
         l_view = linc.rearrange("(p j) e -> p j e", j=J)
+
+        def load_x(h):
+            nc.sync.dma_start(out=xs[h][:], in_=x[4 * h:4 * h + 4].rearrange("b (g p t) c -> p b g (t c)", g=4, p=P, t=4))
+
+        load_x(0)
+        for te in range(3):
+            nc.sync.dma_start(out=rs_whole[te][:], in_=r_view[te // 2, te % 2])
+        for k in range(2):
+            nc.sync.dma_start(out=rs_last[k][:], in_=r_view[1, 1][:, 1024 * k:1024 * (k + 1)])
         for q in range(4):
-            t = keep.tile([P, 4, EDGES], BF16, name="ls%d" % q)
-            nc.sync.dma_start(out=t[:], in_=l_view[:, 4 * q:4 * q + 4, :])
-            ls.append(t)
+            nc.sync.dma_start(out=ls[q][:], in_=l_view[:, 4 * q:4 * q + 4, :])
+        load_x(1)
 
         ewf = keep.tile([P, KW, 4], F32, name="ewf")
         nc.vector.tensor_copy(
@@ -57,69 +101,84 @@ def tile_sgcn_pa_t_kernel(tc, x, rinc, linc, edge_w, out):
             in_=ew_raw[:].rearrange("p u (e k) -> p k u e", e=2),
         )
 
-        x_codes, x_scales = [], []
-        for g in range(G):
-            xg = keep.tile([P, B * C * 4], BF16, name="xg%d" % g, align_bytes=64)
-            nc.vector.tensor_copy(
-                out=xg[:].rearrange("p (b c t) -> p b c t", b=B, c=C),
-                in_=xs[g][:].rearrange("p b (t c) -> p b c t", t=4),
-            )
-            cd = keep.tile([P, B * C], U32, name="xc%d" % g, align_bytes=64)
-            sc = keep.tile([P, B * C], U8, name="xsc%d" % g, align_bytes=64)
-            nc.vector.quantize_mx(out=cd[:].bitcast(FP8X4), scales=sc[:], in_=xg[:])
-            x_codes.append(cd)
-            x_scales.append(sc)
-
         z = [ps_z.tile([P, 4, P], F32, name="z%d" % h) for h in range(2)]
-        for te in range(4):
-            rw = rs[te][:].bitcast(F32)
-            rg = keep.tile([P, G * P * 4], BF16, name="rg%d" % te, align_bytes=64)
-            rgw = rg[:].bitcast(F32).rearrange("p (g e h) -> p g e h", g=G, h=2)
-            for gp in range(2):
-                tp = ps_t.tile([P, 2, 2, P], F32, name="tp")
-                for gg in range(2):
-                    g = 2 * gp + gg
-                    for h in range(2):
-                        nc.tensor.transpose(tp[:, gg, h, :], rw[:, 256 * g + h:256 * (g + 1):2], ident[:])
-                src = tp[:].rearrange("p g h e -> p g e h")
-                if gp == 0:
-                    nc.vector.tensor_copy(out=rgw[:, 0:2], in_=src)
-                else:
-                    nc.scalar.copy(out=rgw[:, 2:4], in_=src)
-            cd = keep.tile([P, G * P], U32, name="rc%d" % te, align_bytes=64)
-            sc = keep.tile([P, G * P], U8, name="rsc%d" % te, align_bytes=64)
-            nc.vector.quantize_mx(out=cd[:].bitcast(FP8X4), scales=sc[:], in_=rg[:])
-            for h in range(2):
-                for g in range(G):
-                    nc.tensor.matmul_mx(
-                        out=z[h][:, te, :],
-                        lhsT=cd[:, P * g:P * (g + 1)].bitcast(FP8X4),
-                        lhsT_scale=sc[:, P * g:P * (g + 1)],
-                        rhs=x_codes[g][:, P * h:P * (h + 1)].bitcast(FP8X4),
-                        rhs_scale=x_scales[g][:, P * h:P * (h + 1)],
-                        start=(g == 0),
-                        stop=(g == G - 1),
-                    )
-
-        l_codes, l_scales = [], []
-        for q in range(4):
-            lw = ls[q][:].bitcast(F32)
-            lg = keep.tile([P, 4 * P * 4], BF16, name="lg%d" % q, align_bytes=64)
-            lgw = lg[:].bitcast(F32).rearrange("p (j n u) -> p j n u", j=4, u=2)
-            for jp in range(2):
-                tp = ps_t.tile([P, 2, 2, P], F32, name="tp")
-                for jj in range(2):
-                    for u in range(2):
-                        nc.tensor.transpose(tp[:, jj, u, :], lw[:, 2 * jp + jj, P * u:P * (u + 1)], ident[:])
-                nc.scalar.copy(out=lgw[:, 2 * jp:2 * jp + 2], in_=tp[:].rearrange("p j u n -> p j n u"))
-            cd = keep.tile([P, 4 * P], U32, name="lc%d" % q, align_bytes=64)
-            sc = keep.tile([P, 4 * P], U8, name="lsc%d" % q, align_bytes=64)
-            nc.vector.quantize_mx(out=cd[:].bitcast(FP8X4), scales=sc[:], in_=lg[:])
-            l_codes.append(cd)
-            l_scales.append(sc)
-
         o_view = out.rearrange("b (p j) w -> b p j w", j=J)
-        for b in range(B):
+        live = {}
+
+        def copy(eng, dst, src):
+            if eng == "V":
+                nc.vector.tensor_copy(out=dst, in_=src)
+            else:
+                nc.scalar.copy(out=dst, in_=src)
+
+        def quant(key, width, src):
+            cd = keep.tile([P, width // 4], U32, name="c_%s_%d_%d" % key, align_bytes=64)
+            sc = keep.tile([P, width // 4], U8, name="s_%s_%d_%d" % key, align_bytes=64)
+            nc.vector.quantize_mx(out=cd[:].bitcast(FP8X4), scales=sc[:], in_=src)
+            live[key] = (cd, sc)
+
+        def op_xr(h):
+            xg = keep.tile([P, 4, P * 4], BF16, name="xg%d" % h, align_bytes=64)
+            for g in range(4):
+                nc.vector.tensor_copy(
+                    out=xg[:, g, :].rearrange("p (b c t) -> p b c t", b=4, c=C),
+                    in_=xs[h][:, :, g, :].rearrange("p b (t c) -> p b c t", t=4),
+                )
+            live[("xg", h)] = xg
+
+        def op_xq(h):
+            quant(("x", h, 0), 2048, live[("xg", h)][:].rearrange("p g w -> p (g w)"))
+
+        def op_tr(te, k):
+            tp = ps.tile([P, 2, 2, P], F32, name="tp", tag="bank")
+            rw = (rs_whole[te][:, 1024 * k:1024 * (k + 1)] if te < 3 else rs_last[k][:]).bitcast(F32)
+            for gg in range(2):
+                for h in range(2):
+                    nc.tensor.transpose(tp[:, gg, h, :], rw[:, 256 * gg + h:256 * (gg + 1):2], ident[:])
+            live[("tr", te, k)] = tp
+
+        def op_cr(te, k, eng):
+            rg = keep.tile([P, 2 * P * 4], BF16, name="rg%d_%d" % (te, k), align_bytes=64)
+            copy(eng, rg[:].bitcast(F32).rearrange("p (g e h) -> p g e h", g=2, h=2),
+                 live[("tr", te, k)][:].rearrange("p g h e -> p g e h"))
+            live[("rg", te, k)] = rg
+
+        def op_rq(te, k):
+            quant(("r", te, k), 1024, live[("rg", te, k)][:])
+
+        def op_z(te, h, k):
+            cd, sc = live[("r", te, k)]
+            xc, xsc = live[("x", h, 0)]
+            for gg in range(2):
+                g = 2 * k + gg
+                nc.tensor.matmul_mx(
+                    out=z[h][:, te, :],
+                    lhsT=cd[:, P * gg:P * (gg + 1)].bitcast(FP8X4),
+                    lhsT_scale=sc[:, P * gg:P * (gg + 1)],
+                    rhs=xc[:, P * g:P * (g + 1)].bitcast(FP8X4),
+                    rhs_scale=xsc[:, P * g:P * (g + 1)],
+                    start=(g == 0),
+                    stop=(g == 3),
+                )
+
+        def op_tl(q, k):
+            tp = ps.tile([P, 2, 2, P], F32, name="tp", tag="bank")
+            lw = ls[q][:].bitcast(F32)
+            for jj in range(2):
+                for u in range(2):
+                    nc.tensor.transpose(tp[:, jj, u, :], lw[:, 2 * k + jj, P * u:P * (u + 1)], ident[:])
+            live[("tl", q, k)] = tp
+
+        def op_cl(q, k, eng):
+            lg = keep.tile([P, 2 * P * 4], BF16, name="lg%d_%d" % (q, k), align_bytes=64)
+            copy(eng, lg[:].bitcast(F32).rearrange("p (j n u) -> p j n u", j=2, u=2),
+                 live[("tl", q, k)][:].rearrange("p j u n -> p j n u"))
+            live[("lg", q, k)] = lg
+
+        def op_lq(q, k):
+            quant(("l", q, k), 1024, live[("lg", q, k)][:])
+
+        def op_m(b):
             mg = keep.tile([P, W * 4], BF16, name="mg%d" % b, align_bytes=64)
             nc.vector.tensor_tensor(
                 out=mg[:].rearrange("p (c k t) -> p c k t", c=C, k=KW),
@@ -127,27 +186,47 @@ def tile_sgcn_pa_t_kernel(tc, x, rinc, linc, edge_w, out):
                 in1=ewf[:].unsqueeze(1).to_broadcast([P, C, KW, 4]),
                 op=mybir.AluOpType.mult,
             )
-            mc = keep.tile([P, W], U32, name="mc%d" % b, align_bytes=64)
-            ms = keep.tile([P, W], U8, name="msc%d" % b, align_bytes=64)
-            nc.vector.quantize_mx(out=mc[:].bitcast(FP8X4), scales=ms[:], in_=mg[:])
-            for half in range(2):
-                st = stage.tile([P, 8, W], F32, name="st")
-                for jq in range(4):
-                    jp = 4 * half + jq
-                    o = ps_o.tile([P, 2, W], F32, name="o")
-                    for jj in range(2):
-                        j = 2 * jp + jj
-                        nc.tensor.matmul_mx(
-                            out=o[:, jj, :],
-                            lhsT=l_codes[j // 4][:, P * (j % 4):P * (j % 4 + 1)].bitcast(FP8X4),
-                            lhsT_scale=l_scales[j // 4][:, P * (j % 4):P * (j % 4 + 1)],
-                            rhs=mc[:].bitcast(FP8X4),
-                            rhs_scale=ms[:],
-                            start=True,
-                            stop=True,
-                        )
-                    if jp in VEC_BANKS:
-                        nc.vector.tensor_copy(out=st[:, 2 * jq:2 * jq + 2, :], in_=o[:])
-                    else:
-                        nc.scalar.copy(out=st[:, 2 * jq:2 * jq + 2, :], in_=o[:])
-                nc.sync.dma_start(out=o_view[b, :, 8 * half:8 * half + 8, :], in_=st[:])
+            live[("mg", b)] = mg
+
+        def op_mq(b):
+            quant(("m", b, 0), 1024, live[("mg", b)][:])
+
+        def op_o(b, jp):
+            o = ps.tile([P, 2, W], F32, name="o", tag="bank")
+            cd, sc = live[("l", jp // 2, jp % 2)]
+            mc, ms = live[("m", b, 0)]
+            for jj in range(2):
+                nc.tensor.matmul_mx(
+                    out=o[:, jj, :],
+                    lhsT=cd[:, P * jj:P * (jj + 1)].bitcast(FP8X4),
+                    lhsT_scale=sc[:, P * jj:P * (jj + 1)],
+                    rhs=mc[:].bitcast(FP8X4),
+                    rhs_scale=ms[:],
+                    start=True,
+                    stop=True,
+                )
+            live[("o", b, jp)] = o
+
+        def group_of(b, jp):
+            j0 = 0
+            for n in STORES[b]:
+                if jp < j0 + n:
+                    return j0, n
+                j0 += n
+            return None
+
+        def op_co(b, jp, eng):
+            j0, n = group_of(b, jp)
+            if ("st", b, j0) not in live:
+                live[("st", b, j0)] = stage.tile([P, 2 * n, W], F32, name="st%d" % n, bufs=ST_BUFS[n])
+            st = live[("st", b, j0)]
+            copy(eng, st[:, 2 * (jp - j0):2 * (jp - j0) + 2, :], live[("o", b, jp)][:])
+
+        def op_st(b, j0):
+            n = group_of(b, j0)[1]
+            nc.sync.dma_start(out=o_view[b, :, 2 * j0:2 * (j0 + n), :], in_=live[("st", b, j0)][:])
+
+        table = {"xr": op_xr, "xq": op_xq, "tr": op_tr, "cr": op_cr, "rq": op_rq, "z": op_z, "tl": op_tl,
+                 "cl": op_cl, "lq": op_lq, "m": op_m, "mq": op_mq, "o": op_o, "co": op_co, "st": op_st}
+        for step in ORDER:
+            table[step[0]](*step[1:])

@@ -15,51 +15,6 @@ W = C * KW
 J = NODES // P
 FLOPS = 2 * EDGES * NODES * B * C + 2 * NODES * EDGES * B * W
 
-STORES = ((1, 1, 2, 2, 2), (2, 2, 4), (4, 4), (4, 4), (4, 4), (4, 4), (4, 4), (4, 4))
-ST_BUFS = {1: 2, 2: 5, 4: 8}
-
-ORDER = (
-    ("xr", 0), ("tr", 0, 0), ("xq", 0), ("cr", 0, 0, "S"), ("tr", 0, 1), ("cr", 0, 1, "V"),
-    ("tr", 1, 0), ("rq", 0, 0), ("cr", 1, 0, "S"), ("tr", 1, 1), ("rq", 0, 1), ("tr", 2, 0),
-    ("rq", 1, 0), ("cr", 1, 1, "S"), ("tr", 2, 1), ("rq", 1, 1), ("cr", 2, 0, "S"), ("cr", 2, 1, "V"),
-    ("tr", 3, 0), ("tr", 3, 1), ("rq", 2, 0), ("cr", 3, 0, "S"), ("rq", 2, 1), ("cr", 3, 1, "S"),
-    ("z", 0, 0, 0), ("rq", 3, 0), ("z", 0, 0, 1), ("z", 1, 0, 0), ("rq", 3, 1), ("z", 1, 0, 1),
-    ("z", 2, 0, 0), ("z", 2, 0, 1), ("z", 3, 0, 0), ("z", 3, 0, 1), ("tl", 0, 0), ("m", 0),
-    ("cl", 0, 0, "S"), ("tl", 0, 1), ("tl", 1, 0), ("tl", 1, 1), ("lq", 0, 0), ("cl", 0, 1, "S"),
-    ("mq", 0), ("tl", 2, 0), ("cl", 1, 0, "S"), ("lq", 0, 1), ("tl", 2, 1), ("o", 0, 0),
-    ("cl", 1, 1, "V"), ("cl", 2, 0, "S"), ("o", 0, 1), ("co", 0, 0, "V"), ("st", 0, 0), ("co", 0, 1, "S"),
-    ("st", 0, 1), ("tl", 3, 0), ("lq", 1, 0), ("tl", 3, 1), ("cl", 2, 1, "S"), ("lq", 1, 1),
-    ("lq", 2, 0), ("o", 0, 2), ("cl", 3, 0, "S"), ("lq", 2, 1), ("o", 0, 3), ("co", 0, 2, "S"),
-    ("m", 1), ("o", 0, 4), ("o", 0, 5), ("co", 0, 3, "S"), ("st", 0, 2), ("lq", 3, 0),
-    ("cl", 3, 1, "S"), ("co", 0, 4, "V"), ("co", 0, 5, "S"), ("st", 0, 4), ("o", 0, 6), ("lq", 3, 1),
-    ("mq", 1), ("co", 0, 6, "S"), ("o", 0, 7), ("m", 2), ("co", 0, 7, "S"), ("st", 0, 6),
-    ("o", 1, 0), ("o", 1, 1), ("co", 1, 0, "S"), ("o", 1, 2), ("co", 1, 1, "V"), ("st", 1, 0),
-    ("o", 1, 3), ("co", 1, 2, "S"), ("o", 1, 4), ("co", 1, 3, "V"), ("st", 1, 2), ("o", 1, 5),
-    ("o", 1, 6), ("co", 1, 4, "S"), ("mq", 2), ("o", 1, 7), ("co", 1, 5, "V"), ("co", 1, 6, "S"),
-    ("o", 2, 0), ("co", 1, 7, "S"), ("st", 1, 4), ("co", 2, 0, "V"), ("o", 2, 1), ("o", 2, 2),
-    ("co", 2, 1, "S"), ("o", 2, 3), ("co", 2, 2, "V"), ("o", 2, 4), ("co", 2, 3, "S"), ("st", 2, 0),
-    ("o", 2, 5), ("m", 3), ("o", 2, 6), ("co", 2, 4, "S"), ("o", 2, 7), ("co", 2, 5, "S"),
-    ("mq", 3), ("co", 2, 6, "S"), ("co", 2, 7, "V"), ("st", 2, 4), ("o", 3, 0), ("co", 3, 0, "S"),
-    ("xr", 1), ("o", 3, 1), ("o", 3, 2), ("co", 3, 1, "S"), ("o", 3, 3), ("o", 3, 4),
-    ("o", 3, 5), ("xq", 1), ("co", 3, 2, "S"), ("o", 3, 6), ("o", 3, 7), ("co", 3, 3, "S"),
-    ("st", 3, 0), ("co", 3, 4, "V"), ("z", 0, 1, 0), ("co", 3, 5, "S"), ("z", 0, 1, 1), ("co", 3, 6, "V"),
-    ("z", 1, 1, 0), ("z", 1, 1, 1), ("co", 3, 7, "S"), ("st", 3, 4), ("z", 2, 1, 0), ("z", 2, 1, 1),
-    ("z", 3, 1, 0), ("z", 3, 1, 1), ("m", 4), ("mq", 4), ("m", 5), ("o", 4, 0),
-    ("co", 4, 0, "S"), ("o", 4, 1), ("o", 4, 2), ("co", 4, 1, "V"), ("co", 4, 2, "S"), ("o", 4, 3),
-    ("o", 4, 4), ("co", 4, 3, "V"), ("st", 4, 0), ("o", 4, 5), ("co", 4, 4, "S"), ("o", 4, 6),
-    ("mq", 5), ("o", 4, 7), ("co", 4, 5, "S"), ("co", 4, 6, "V"), ("co", 4, 7, "S"), ("st", 4, 4),
-    ("o", 5, 0), ("co", 5, 0, "V"), ("o", 5, 1), ("co", 5, 1, "S"), ("o", 5, 2), ("o", 5, 3),
-    ("co", 5, 2, "V"), ("co", 5, 3, "S"), ("st", 5, 0), ("o", 5, 4), ("o", 5, 5), ("m", 6),
-    ("o", 5, 6), ("co", 5, 4, "S"), ("o", 5, 7), ("co", 5, 5, "S"), ("mq", 6), ("co", 5, 6, "S"),
-    ("co", 5, 7, "V"), ("st", 5, 4), ("o", 6, 0), ("co", 6, 0, "S"), ("o", 6, 1), ("m", 7),
-    ("o", 6, 2), ("co", 6, 1, "S"), ("o", 6, 3), ("o", 6, 4), ("co", 6, 2, "V"), ("o", 6, 5),
-    ("co", 6, 3, "S"), ("st", 6, 0), ("o", 6, 6), ("mq", 7), ("o", 6, 7), ("co", 6, 4, "S"),
-    ("co", 6, 5, "V"), ("co", 6, 6, "S"), ("o", 7, 0), ("co", 6, 7, "V"), ("st", 6, 4), ("o", 7, 1),
-    ("co", 7, 0, "S"), ("o", 7, 2), ("co", 7, 1, "V"), ("o", 7, 3), ("co", 7, 2, "S"), ("o", 7, 4),
-    ("co", 7, 3, "V"), ("st", 7, 0), ("o", 7, 5), ("co", 7, 4, "S"), ("o", 7, 6), ("o", 7, 7),
-    ("co", 7, 5, "V"), ("co", 7, 6, "S"), ("co", 7, 7, "V"), ("st", 7, 4),
-)
-
 
 def tile_sgcn_pa_t_kernel(tc, x, rinc, linc, edge_w, out):
     nc = tc.nc
@@ -75,9 +30,8 @@ def tile_sgcn_pa_t_kernel(tc, x, rinc, linc, edge_w, out):
 
         ew_raw = keep.tile([P, 2, 2 * KW], BF16, name="ew_raw")
         nc.scalar.dma_start(out=ew_raw[:], in_=edge_w.rearrange("(u p e) k -> p u (e k)", u=2, p=P, e=2))
-
         xs = [keep.tile([P, 4, 4, 4 * C], BF16, name="xs%d" % h) for h in range(2)]
-        rs_whole = [keep.tile([P, NODES], BF16, name="rs%d" % te) for te in range(3)]
+        rs = [keep.tile([P, NODES], BF16, name="rs%d" % te) for te in range(3)]
         rs_last = [keep.tile([P, NODES // 2], BF16, name="rs3_%d" % k) for k in range(2)]
         ls = [keep.tile([P, 4, EDGES], BF16, name="ls%d" % q) for q in range(4)]
         r_view = rinc.rearrange("(u p e) n -> u e p n", u=2, p=P, e=2)
@@ -88,7 +42,7 @@ def tile_sgcn_pa_t_kernel(tc, x, rinc, linc, edge_w, out):
 
         load_x(0)
         for te in range(3):
-            nc.sync.dma_start(out=rs_whole[te][:], in_=r_view[te // 2, te % 2])
+            nc.sync.dma_start(out=rs[te][:], in_=r_view[te // 2, te % 2])
         for k in range(2):
             nc.sync.dma_start(out=rs_last[k][:], in_=r_view[1, 1][:, 1024 * k:1024 * (k + 1)])
         for q in range(4):
@@ -101,132 +55,147 @@ def tile_sgcn_pa_t_kernel(tc, x, rinc, linc, edge_w, out):
             in_=ew_raw[:].rearrange("p u (e k) -> p k u e", e=2),
         )
 
-        z = [ps_z.tile([P, 4, P], F32, name="z%d" % h) for h in range(2)]
-        o_view = out.rearrange("b (p j) w -> b p j w", j=J)
-        live = {}
-
-        def copy(eng, dst, src):
-            if eng == "V":
+        def empty_bank(on_vector, dst, src):
+            if on_vector:
                 nc.vector.tensor_copy(out=dst, in_=src)
             else:
                 nc.scalar.copy(out=dst, in_=src)
 
-        def quant(key, width, src):
-            cd = keep.tile([P, width // 4], U32, name="c_%s_%d_%d" % key, align_bytes=64)
-            sc = keep.tile([P, width // 4], U8, name="s_%s_%d_%d" % key, align_bytes=64)
-            nc.vector.quantize_mx(out=cd[:].bitcast(FP8X4), scales=sc[:], in_=src)
-            live[key] = (cd, sc)
+        def quantise(name, src, width):
+            codes = keep.tile([P, width // 4], U32, name="c_" + name, align_bytes=64)
+            scales = keep.tile([P, width // 4], U8, name="s_" + name, align_bytes=64)
+            nc.vector.quantize_mx(out=codes[:].bitcast(FP8X4), scales=scales[:], in_=src)
+            return codes, scales
 
-        def op_xr(h):
+        x_q = [None, None]
+
+        def prepare_x(h):
             xg = keep.tile([P, 4, P * 4], BF16, name="xg%d" % h, align_bytes=64)
             for g in range(4):
                 nc.vector.tensor_copy(
                     out=xg[:, g, :].rearrange("p (b c t) -> p b c t", b=4, c=C),
                     in_=xs[h][:, :, g, :].rearrange("p b (t c) -> p b c t", t=4),
                 )
-            live[("xg", h)] = xg
+            x_q[h] = quantise("x%d" % h, xg[:].rearrange("p g w -> p (g w)"), 2048)
 
-        def op_xq(h):
-            quant(("x", h, 0), 2048, live[("xg", h)][:].rearrange("p g w -> p (g w)"))
+        prepare_x(0)
 
-        def op_tr(te, k):
-            tp = ps.tile([P, 2, 2, P], F32, name="tp", tag="bank")
-            rw = (rs_whole[te][:, 1024 * k:1024 * (k + 1)] if te < 3 else rs_last[k][:]).bitcast(F32)
+        r_grouped = [None] * 8
+        r_q = [None] * 8
+
+        def quantise_r(i):
+            r_q[i] = quantise("r%d" % i, r_grouped[i][:], 1024)
+
+        for i in range(8):
+            te, k = i // 2, i % 2
+            words = (rs[te][:, 1024 * k:1024 * (k + 1)] if te < 3 else rs_last[k][:]).bitcast(F32)
+            bank = ps.tile([P, 2, 2, P], F32, name="bank")
             for gg in range(2):
                 for h in range(2):
-                    nc.tensor.transpose(tp[:, gg, h, :], rw[:, 256 * gg + h:256 * (gg + 1):2], ident[:])
-            live[("tr", te, k)] = tp
+                    nc.tensor.transpose(bank[:, gg, h, :], words[:, 256 * gg + h:256 * (gg + 1):2], ident[:])
+            r_grouped[i] = keep.tile([P, 2 * P * 4], BF16, name="rg%d" % i, align_bytes=64)
+            empty_bank(i in (1, 5), r_grouped[i][:].bitcast(F32).rearrange("p (g e h) -> p g e h", g=2, h=2),
+                       bank[:].rearrange("p g h e -> p g e h"))
+            if i >= 1:
+                quantise_r(i - 1)
+        quantise_r(7)
 
-        def op_cr(te, k, eng):
-            rg = keep.tile([P, 2 * P * 4], BF16, name="rg%d_%d" % (te, k), align_bytes=64)
-            copy(eng, rg[:].bitcast(F32).rearrange("p (g e h) -> p g e h", g=2, h=2),
-                 live[("tr", te, k)][:].rearrange("p g h e -> p g e h"))
-            live[("rg", te, k)] = rg
+        z = [ps_z.tile([P, 4, P], F32, name="z%d" % h) for h in range(2)]
 
-        def op_rq(te, k):
-            quant(("r", te, k), 1024, live[("rg", te, k)][:])
+        def first_matmul(h):
+            for te in range(4):
+                for g in range(4):
+                    codes, scales = r_q[2 * te + g // 2]
+                    cols = slice(P * (g % 2), P * (g % 2 + 1))
+                    nc.tensor.matmul_mx(
+                        out=z[h][:, te, :],
+                        lhsT=codes[:, cols].bitcast(FP8X4),
+                        lhsT_scale=scales[:, cols],
+                        rhs=x_q[h][0][:, P * g:P * (g + 1)].bitcast(FP8X4),
+                        rhs_scale=x_q[h][1][:, P * g:P * (g + 1)],
+                        start=(g == 0),
+                        stop=(g == 3),
+                    )
 
-        def op_z(te, h, k):
-            cd, sc = live[("r", te, k)]
-            xc, xsc = live[("x", h, 0)]
-            for gg in range(2):
-                g = 2 * k + gg
-                nc.tensor.matmul_mx(
-                    out=z[h][:, te, :],
-                    lhsT=cd[:, P * gg:P * (gg + 1)].bitcast(FP8X4),
-                    lhsT_scale=sc[:, P * gg:P * (gg + 1)],
-                    rhs=xc[:, P * g:P * (g + 1)].bitcast(FP8X4),
-                    rhs_scale=xsc[:, P * g:P * (g + 1)],
-                    start=(g == 0),
-                    stop=(g == 3),
-                )
+        first_matmul(0)
 
-        def op_tl(q, k):
-            tp = ps.tile([P, 2, 2, P], F32, name="tp", tag="bank")
-            lw = ls[q][:].bitcast(F32)
+        l_bank = [None] * 8
+        l_grouped = [None] * 8
+        l_q = [None] * 8
+
+        def transpose_l(i):
+            words = ls[i // 2][:].bitcast(F32)
+            l_bank[i] = ps.tile([P, 2, 2, P], F32, name="bank")
             for jj in range(2):
                 for u in range(2):
-                    nc.tensor.transpose(tp[:, jj, u, :], lw[:, 2 * k + jj, P * u:P * (u + 1)], ident[:])
-            live[("tl", q, k)] = tp
+                    nc.tensor.transpose(l_bank[i][:, jj, u, :], words[:, 2 * (i % 2) + jj, P * u:P * (u + 1)], ident[:])
 
-        def op_cl(q, k, eng):
-            lg = keep.tile([P, 2 * P * 4], BF16, name="lg%d_%d" % (q, k), align_bytes=64)
-            copy(eng, lg[:].bitcast(F32).rearrange("p (j n u) -> p j n u", j=2, u=2),
-                 live[("tl", q, k)][:].rearrange("p j u n -> p j n u"))
-            live[("lg", q, k)] = lg
+        def copy_l(i):
+            l_grouped[i] = keep.tile([P, 2 * P * 4], BF16, name="lg%d" % i, align_bytes=64)
+            empty_bank(False, l_grouped[i][:].bitcast(F32).rearrange("p (j n u) -> p j n u", j=2, u=2),
+                       l_bank[i][:].rearrange("p j u n -> p j n u"))
 
-        def op_lq(q, k):
-            quant(("l", q, k), 1024, live[("lg", q, k)][:])
+        def quantise_l(i):
+            l_q[i] = quantise("l%d" % i, l_grouped[i][:], 1024)
 
-        def op_m(b):
-            mg = keep.tile([P, W * 4], BF16, name="mg%d" % b, align_bytes=64)
+        m_grouped = [None] * B
+        m_q = [None] * B
+
+        def messages(b):
+            m_grouped[b] = keep.tile([P, W * 4], BF16, name="mg%d" % b, align_bytes=64)
             nc.vector.tensor_tensor(
-                out=mg[:].rearrange("p (c k t) -> p c k t", c=C, k=KW),
+                out=m_grouped[b][:].rearrange("p (c k t) -> p c k t", c=C, k=KW),
                 in0=z[b // 4][:, :, C * (b % 4):C * (b % 4 + 1)].rearrange("p t c -> p c t").unsqueeze(2).to_broadcast([P, C, KW, 4]),
                 in1=ewf[:].unsqueeze(1).to_broadcast([P, C, KW, 4]),
                 op=mybir.AluOpType.mult,
             )
-            live[("mg", b)] = mg
 
-        def op_mq(b):
-            quant(("m", b, 0), 1024, live[("mg", b)][:])
+        def quantise_m(b):
+            m_q[b] = quantise("m%d" % b, m_grouped[b][:], 1024)
 
-        def op_o(b, jp):
-            o = ps.tile([P, 2, W], F32, name="o", tag="bank")
-            cd, sc = live[("l", jp // 2, jp % 2)]
-            mc, ms = live[("m", b, 0)]
-            for jj in range(2):
-                nc.tensor.matmul_mx(
-                    out=o[:, jj, :],
-                    lhsT=cd[:, P * jj:P * (jj + 1)].bitcast(FP8X4),
-                    lhsT_scale=sc[:, P * jj:P * (jj + 1)],
-                    rhs=mc[:].bitcast(FP8X4),
-                    rhs_scale=ms[:],
-                    start=True,
-                    stop=True,
-                )
-            live[("o", b, jp)] = o
+        for i in range(6):
+            transpose_l(i)
+        for i in range(4):
+            copy_l(i)
+        messages(0)
+        quantise_l(0)
+        quantise_m(0)
+        quantise_l(1)
 
-        def group_of(b, jp):
-            j0 = 0
-            for n in STORES[b]:
-                if jp < j0 + n:
-                    return j0, n
-                j0 += n
-            return None
-
-        def op_co(b, jp, eng):
-            j0, n = group_of(b, jp)
-            if ("st", b, j0) not in live:
-                live[("st", b, j0)] = stage.tile([P, 2 * n, W], F32, name="st%d" % n, bufs=ST_BUFS[n])
-            st = live[("st", b, j0)]
-            copy(eng, st[:, 2 * (jp - j0):2 * (jp - j0) + 2, :], live[("o", b, jp)][:])
-
-        def op_st(b, j0):
-            n = group_of(b, j0)[1]
-            nc.sync.dma_start(out=o_view[b, :, 2 * j0:2 * (j0 + n), :], in_=live[("st", b, j0)][:])
-
-        table = {"xr": op_xr, "xq": op_xq, "tr": op_tr, "cr": op_cr, "rq": op_rq, "z": op_z, "tl": op_tl,
-                 "cl": op_cl, "lq": op_lq, "m": op_m, "mq": op_mq, "o": op_o, "co": op_co, "st": op_st}
-        for step in ORDER:
-            table[step[0]](*step[1:])
+        o_view = out.rearrange("b (p j) w -> b p j w", j=J)
+        for b in range(B):
+            i = 0
+            for n in ((2, 2, 2, 2) if b == 0 else (4, 4)):
+                st = stage.tile([P, 2 * n, W], F32, name="st%d" % n, bufs={2: 4, 4: 8}[n])
+                for s in range(n):
+                    acc = ps.tile([P, 2, W], F32, name="bank")
+                    for jj in range(2):
+                        nc.tensor.matmul_mx(
+                            out=acc[:, jj, :],
+                            lhsT=l_q[i][0][:, P * jj:P * (jj + 1)].bitcast(FP8X4),
+                            lhsT_scale=l_q[i][1][:, P * jj:P * (jj + 1)],
+                            rhs=m_q[b][0][:].bitcast(FP8X4),
+                            rhs_scale=m_q[b][1][:],
+                            start=True,
+                            stop=True,
+                        )
+                    if b == 0:
+                        if i + 6 < 8:
+                            transpose_l(i + 6)
+                        if i + 4 < 8:
+                            copy_l(i + 4)
+                        if i + 2 < 8:
+                            quantise_l(i + 2)
+                    elif i == 1 and b + 1 < B:
+                        messages(b + 1)
+                        quantise_m(b + 1)
+                    if b == 2 and i == 2:
+                        prepare_x(1)
+                    if b == 2 and i == 6:
+                        first_matmul(1)
+                    empty_bank(i in ((0, 4) if b == 0 else (2, 4, 6)), st[:, 2 * s:2 * s + 2, :], acc[:])
+                    if b == 0 and i == 3:
+                        messages(1)
+                        quantise_m(1)
+                    i += 1
+                nc.sync.dma_start(out=o_view[b, :, 2 * (i - n):2 * i, :], in_=st[:])

@@ -23,7 +23,6 @@ def tile_sgcn_pa_t_kernel(tc, x, rinc, linc, edge_w, out):
         stage = ctx.enter_context(tc.tile_pool(name="stage", bufs=1))
         ps_z = ctx.enter_context(tc.psum_pool(name="ps_z", bufs=1))
         ps = ctx.enter_context(tc.psum_pool(name="ps", bufs=6))
-        ctx.enter_context(tc.manual_schedule())
 
         ident = keep.tile([P, P], F32, name="ident")
         make_identity(nc, ident[:])

@@ -10,10 +10,22 @@ U32 = mybir.dt.uint32
 U8 = mybir.dt.uint8
 
 P = 128
-B, NODES, EDGES, C, KW = 8, 2048, 512, 32, 8
-W = C * KW
-J = NODES // P
-FLOPS = 2 * EDGES * NODES * B * C + 2 * NODES * EDGES * B * W
+PACK = 4
+SIGNALS, NODES, EDGES, CHANNELS, KERNELS = 8, 2048, 512, 32, 8
+WIDTH = CHANNELS * KERNELS
+NODE_PASSES = NODES // (P * PACK)
+EDGE_TILES = EDGES // P
+NODE_TILES = NODES // P
+BANKS = NODE_TILES // 2
+
+FLOPS = 2 * EDGES * NODES * SIGNALS * CHANNELS + 2 * NODES * EDGES * SIGNALS * WIDTH
+
+X_GROUPS = ((0, 2), (2, 6), (6, 8))
+
+STORE_BANKS = ((1, 1, 2, 2, 2), (2, 2, 4)) + ((4, 4),) * 6
+STAGE_BUFS = {1: 2, 2: 5, 4: 8}
+
+AHEAD_TRANSPOSE, AHEAD_COPY, AHEAD_QUANTISE = 6, 5, 2
 
 
 def tile_sgcn_pa_t_kernel(tc, x, rinc, linc, edge_w, out):
@@ -21,37 +33,49 @@ def tile_sgcn_pa_t_kernel(tc, x, rinc, linc, edge_w, out):
     with ExitStack() as ctx:
         keep = ctx.enter_context(tc.tile_pool(name="keep", bufs=1))
         stage = ctx.enter_context(tc.tile_pool(name="stage", bufs=1))
-        ps_z = ctx.enter_context(tc.psum_pool(name="ps_z", bufs=1))
-        ps = ctx.enter_context(tc.psum_pool(name="ps", bufs=6))
+        z_pool = ctx.enter_context(tc.psum_pool(name="z_pool", bufs=2))
+        bank_pool = ctx.enter_context(tc.psum_pool(name="bank_pool", bufs=6))
+        ctx.enter_context(tc.manual_schedule())
 
-        ident = keep.tile([P, P], F32, name="ident")
-        make_identity(nc, ident[:])
+        identity = keep.tile([P, P], F32, name="identity")
+        make_identity(nc, identity[:])
 
-        ew_raw = keep.tile([P, 2, 2 * KW], BF16, name="ew_raw")
-        nc.scalar.dma_start(out=ew_raw[:], in_=edge_w.rearrange("(u p e) k -> p u (e k)", u=2, p=P, e=2))
-        xs = [keep.tile([P, 4, 4, 4 * C], BF16, name="xs%d" % h) for h in range(2)]
-        rs = [keep.tile([P, NODES], BF16, name="rs%d" % te) for te in range(3)]
-        rs_last = [keep.tile([P, NODES // 2], BF16, name="rs3_%d" % k) for k in range(2)]
-        ls = [keep.tile([P, 4, EDGES], BF16, name="ls%d" % q) for q in range(4)]
-        r_view = rinc.rearrange("(u p e) n -> u e p n", u=2, p=P, e=2)
-        l_view = linc.rearrange("(p j) e -> p j e", j=J)
+        edge_w_rows = keep.tile([P, 2, 2 * KERNELS], BF16, name="edge_w_rows")
+        nc.scalar.dma_start(out=edge_w_rows[:], in_=edge_w.rearrange("(u p e) k -> p u (e k)", u=2, p=P, e=2))
+
+        x_rows = [keep.tile([P, hi - lo, NODE_PASSES, PACK * CHANNELS], BF16, name="x_rows%d" % lo) for lo, hi in X_GROUPS]
+        x_grouped = [
+            keep.tile([P, NODE_PASSES, P * PACK], BF16, name="x_grouped%d" % lo, align_bytes=64) for lo, hi in X_GROUPS
+        ]
+        rinc_rows = [keep.tile([P, NODES], BF16, name="rinc_rows%d" % t) for t in range(EDGE_TILES - 1)]
+        rinc_last = [keep.tile([P, NODES // 2], BF16, name="rinc_last%d" % half) for half in range(2)]
+        linc_rows = [keep.tile([P, 4, EDGES], BF16, name="linc_rows%d" % q) for q in range(NODE_TILES // 4)]
+        rinc_tiles = rinc.rearrange("(u p e) n -> u e p n", u=2, p=P, e=2)
+        linc_tiles = linc.rearrange("(p j) e -> p j e", j=NODE_TILES)
 
         def load_x(h):
-            nc.sync.dma_start(out=xs[h][:], in_=x[4 * h:4 * h + 4].rearrange("b (g p t) c -> p b g (t c)", g=4, p=P, t=4))
+            lo, hi = X_GROUPS[h]
+            if hi - lo < 4:
+                nc.gpsimd.memset(x_grouped[h][:], 0.0)
+            nc.sync.dma_start(
+                out=x_rows[h][:],
+                in_=x[lo:hi].rearrange("b (g p t) c -> p b g (t c)", g=NODE_PASSES, p=P, t=PACK),
+            )
 
         load_x(0)
-        for te in range(3):
-            nc.sync.dma_start(out=rs[te][:], in_=r_view[te // 2, te % 2])
-        for k in range(2):
-            nc.sync.dma_start(out=rs_last[k][:], in_=r_view[1, 1][:, 1024 * k:1024 * (k + 1)])
-        for q in range(4):
-            nc.sync.dma_start(out=ls[q][:], in_=l_view[:, 4 * q:4 * q + 4, :])
+        for t in range(EDGE_TILES - 1):
+            nc.sync.dma_start(out=rinc_rows[t][:], in_=rinc_tiles[t // 2, t % 2])
+        for half in range(2):
+            nc.sync.dma_start(out=rinc_last[half][:], in_=rinc_tiles[1, 1][:, 1024 * half:1024 * (half + 1)])
+        for q in range(NODE_TILES // 4):
+            nc.sync.dma_start(out=linc_rows[q][:], in_=linc_tiles[:, 4 * q:4 * q + 4, :])
         load_x(1)
+        load_x(2)
 
-        ewf = keep.tile([P, KW, 4], F32, name="ewf")
+        edge_w_f32 = keep.tile([P, KERNELS, PACK], F32, name="edge_w_f32")
         nc.vector.tensor_copy(
-            out=ewf[:].rearrange("p k (u e) -> p k u e", u=2),
-            in_=ew_raw[:].rearrange("p u (e k) -> p k u e", e=2),
+            out=edge_w_f32[:].rearrange("p k (u e) -> p k u e", u=2),
+            in_=edge_w_rows[:].rearrange("p u (e k) -> p k u e", e=2),
         )
 
         def empty_bank(on_vector, dst, src):
@@ -60,141 +84,158 @@ def tile_sgcn_pa_t_kernel(tc, x, rinc, linc, edge_w, out):
             else:
                 nc.scalar.copy(out=dst, in_=src)
 
-        def quantise(name, src, width):
-            codes = keep.tile([P, width // 4], U32, name="c_" + name, align_bytes=64)
-            scales = keep.tile([P, width // 4], U8, name="s_" + name, align_bytes=64)
-            nc.vector.quantize_mx(out=codes[:].bitcast(FP8X4), scales=scales[:], in_=src)
+        def quantise(name, grouped, width):
+            codes = keep.tile([P, width // PACK], U32, name="codes_" + name, align_bytes=64)
+            scales = keep.tile([P, width // PACK], U8, name="scales_" + name, align_bytes=64)
+            nc.vector.quantize_mx(out=codes[:].bitcast(FP8X4), scales=scales[:], in_=grouped)
             return codes, scales
 
-        x_q = [None, None]
+        x_mx = [None] * len(X_GROUPS)
 
         def prepare_x(h):
-            xg = keep.tile([P, 4, P * 4], BF16, name="xg%d" % h, align_bytes=64)
-            for g in range(4):
+            lo, hi = X_GROUPS[h]
+            for g in range(NODE_PASSES):
+                filled = x_grouped[h][:, g, 0:(hi - lo) * CHANNELS * PACK]
                 nc.vector.tensor_copy(
-                    out=xg[:, g, :].rearrange("p (b c t) -> p b c t", b=4, c=C),
-                    in_=xs[h][:, :, g, :].rearrange("p b (t c) -> p b c t", t=4),
+                    out=filled.rearrange("p (b c t) -> p b c t", b=hi - lo, c=CHANNELS),
+                    in_=x_rows[h][:, :, g, :].rearrange("p b (t c) -> p b c t", t=PACK),
                 )
-            x_q[h] = quantise("x%d" % h, xg[:].rearrange("p g w -> p (g w)"), 2048)
+            x_mx[h] = quantise("x%d" % h, x_grouped[h][:].rearrange("p g w -> p (g w)"), NODE_PASSES * P * PACK)
 
         prepare_x(0)
 
-        r_grouped = [None] * 8
-        r_q = [None] * 8
+        rinc_grouped = [None] * (2 * EDGE_TILES)
+        rinc_mx = [None] * (2 * EDGE_TILES)
 
-        def quantise_r(i):
-            r_q[i] = quantise("r%d" % i, r_grouped[i][:], 1024)
+        def quantise_rinc(i):
+            rinc_mx[i] = quantise("rinc%d" % i, rinc_grouped[i][:], 2 * P * PACK)
 
-        for i in range(8):
-            te, k = i // 2, i % 2
-            words = (rs[te][:, 1024 * k:1024 * (k + 1)] if te < 3 else rs_last[k][:]).bitcast(F32)
-            bank = ps.tile([P, 2, 2, P], F32, name="bank")
-            for gg in range(2):
-                for h in range(2):
-                    nc.tensor.transpose(bank[:, gg, h, :], words[:, 256 * gg + h:256 * (gg + 1):2], ident[:])
-            r_grouped[i] = keep.tile([P, 2 * P * 4], BF16, name="rg%d" % i, align_bytes=64)
-            empty_bank(i in (1, 5), r_grouped[i][:].bitcast(F32).rearrange("p (g e h) -> p g e h", g=2, h=2),
-                       bank[:].rearrange("p g h e -> p g e h"))
+        for i in range(2 * EDGE_TILES):
+            t, half = i // 2, i % 2
+            rows = rinc_rows[t][:, 1024 * half:1024 * (half + 1)] if t < EDGE_TILES - 1 else rinc_last[half][:]
+            words = rows.bitcast(F32)
+            bank = bank_pool.tile([P, 2, 2, P], F32, name="bank")
+            for g in range(2):
+                for pair in range(2):
+                    nc.tensor.transpose(bank[:, g, pair, :], words[:, 256 * g + pair:256 * (g + 1):2], identity[:])
+            rinc_grouped[i] = keep.tile([P, 2 * P * PACK], BF16, name="rinc_grouped%d" % i, align_bytes=64)
+            empty_bank(
+                i % 4 == 1,
+                rinc_grouped[i][:].bitcast(F32).rearrange("p (g e pair) -> p g e pair", g=2, pair=2),
+                bank[:].rearrange("p g pair e -> p g e pair"),
+            )
             if i >= 1:
-                quantise_r(i - 1)
-        quantise_r(7)
+                quantise_rinc(i - 1)
+        quantise_rinc(2 * EDGE_TILES - 1)
 
-        z = [ps_z.tile([P, 4, P], F32, name="z%d" % h) for h in range(2)]
+        z = [None] * len(X_GROUPS)
 
         def first_matmul(h):
-            for te in range(4):
-                for g in range(4):
-                    codes, scales = r_q[2 * te + g // 2]
-                    cols = slice(P * (g % 2), P * (g % 2 + 1))
+            z[h] = z_pool.tile([P, EDGE_TILES, P], F32, name="z")
+            for t in range(EDGE_TILES):
+                for g in range(NODE_PASSES):
+                    codes, scales = rinc_mx[2 * t + g // 2]
+                    edges = slice(P * (g % 2), P * (g % 2 + 1))
                     nc.tensor.matmul_mx(
-                        out=z[h][:, te, :],
-                        lhsT=codes[:, cols].bitcast(FP8X4),
-                        lhsT_scale=scales[:, cols],
-                        rhs=x_q[h][0][:, P * g:P * (g + 1)].bitcast(FP8X4),
-                        rhs_scale=x_q[h][1][:, P * g:P * (g + 1)],
+                        out=z[h][:, t, :],
+                        lhsT=codes[:, edges].bitcast(FP8X4),
+                        lhsT_scale=scales[:, edges],
+                        rhs=x_mx[h][0][:, P * g:P * (g + 1)].bitcast(FP8X4),
+                        rhs_scale=x_mx[h][1][:, P * g:P * (g + 1)],
                         start=(g == 0),
-                        stop=(g == 3),
+                        stop=(g == NODE_PASSES - 1),
                     )
 
-        first_matmul(0)
+        linc_bank = [None] * BANKS
+        linc_grouped = [None] * BANKS
+        linc_mx = [None] * BANKS
 
-        l_bank = [None] * 8
-        l_grouped = [None] * 8
-        l_q = [None] * 8
-
-        def transpose_l(i):
-            words = ls[i // 2][:].bitcast(F32)
-            l_bank[i] = ps.tile([P, 2, 2, P], F32, name="bank")
-            for jj in range(2):
+        def transpose_linc(i):
+            words = linc_rows[i // 2][:].bitcast(F32)
+            linc_bank[i] = bank_pool.tile([P, 2, 2, P], F32, name="bank")
+            for j in range(2):
                 for u in range(2):
-                    nc.tensor.transpose(l_bank[i][:, jj, u, :], words[:, 2 * (i % 2) + jj, P * u:P * (u + 1)], ident[:])
+                    nc.tensor.transpose(linc_bank[i][:, j, u, :], words[:, 2 * (i % 2) + j, P * u:P * (u + 1)], identity[:])
 
-        def copy_l(i):
-            l_grouped[i] = keep.tile([P, 2 * P * 4], BF16, name="lg%d" % i, align_bytes=64)
-            empty_bank(False, l_grouped[i][:].bitcast(F32).rearrange("p (j n u) -> p j n u", j=2, u=2),
-                       l_bank[i][:].rearrange("p j u n -> p j n u"))
-
-        def quantise_l(i):
-            l_q[i] = quantise("l%d" % i, l_grouped[i][:], 1024)
-
-        m_grouped = [None] * B
-        m_q = [None] * B
-
-        def messages(b):
-            m_grouped[b] = keep.tile([P, W * 4], BF16, name="mg%d" % b, align_bytes=64)
-            nc.vector.tensor_tensor(
-                out=m_grouped[b][:].rearrange("p (c k t) -> p c k t", c=C, k=KW),
-                in0=z[b // 4][:, :, C * (b % 4):C * (b % 4 + 1)].rearrange("p t c -> p c t").unsqueeze(2).to_broadcast([P, C, KW, 4]),
-                in1=ewf[:].unsqueeze(1).to_broadcast([P, C, KW, 4]),
-                op=mybir.AluOpType.mult,
+        def copy_linc(i):
+            linc_grouped[i] = keep.tile([P, 2 * P * PACK], BF16, name="linc_grouped%d" % i, align_bytes=64)
+            empty_bank(
+                i == BANKS - 1,
+                linc_grouped[i][:].bitcast(F32).rearrange("p (j n u) -> p j n u", j=2, u=2),
+                linc_bank[i][:].rearrange("p j u n -> p j n u"),
             )
 
-        def quantise_m(b):
-            m_q[b] = quantise("m%d" % b, m_grouped[b][:], 1024)
+        def quantise_linc(i):
+            linc_mx[i] = quantise("linc%d" % i, linc_grouped[i][:], 2 * P * PACK)
 
-        for i in range(6):
-            transpose_l(i)
-        for i in range(4):
-            copy_l(i)
-        messages(0)
-        quantise_l(0)
-        quantise_m(0)
-        quantise_l(1)
+        m_mx = [None] * SIGNALS
 
-        o_view = out.rearrange("b (p j) w -> b p j w", j=J)
-        for b in range(B):
+        def messages(b):
+            h = [lo <= b < hi for lo, hi in X_GROUPS].index(True)
+            first = CHANNELS * (b - X_GROUPS[h][0])
+            shape = [P, CHANNELS, KERNELS, PACK]
+            grouped = keep.tile([P, WIDTH * PACK], BF16, name="m_grouped%d" % b, align_bytes=64)
+            nc.vector.tensor_tensor(
+                out=grouped[:].rearrange("p (c k t) -> p c k t", c=CHANNELS, k=KERNELS),
+                in0=z[h][:, :, first:first + CHANNELS].rearrange("p t c -> p c t").unsqueeze(2).to_broadcast(shape),
+                in1=edge_w_f32[:].unsqueeze(1).to_broadcast(shape),
+                op=mybir.AluOpType.mult,
+            )
+            return grouped
+
+        def quantise_messages(b, grouped):
+            m_mx[b] = quantise("m%d" % b, grouped[:], WIDTH * PACK)
+
+        transpose_linc(0)
+        first_matmul(0)
+        for i in range(1, AHEAD_TRANSPOSE):
+            transpose_linc(i)
+        for i in range(AHEAD_COPY):
+            copy_linc(i)
+        m_grouped = messages(0)
+        quantise_linc(0)
+        quantise_messages(0, m_grouped)
+        for i in range(1, AHEAD_QUANTISE):
+            quantise_linc(i)
+
+        out_tiles = out.rearrange("b (p j) w -> b p j w", j=NODE_TILES)
+        group_starts = [lo for lo, hi in X_GROUPS]
+        for b in range(SIGNALS):
+            new_group = b + 1 in group_starts
+            if b == 0:
+                on_vector = ()
+            elif new_group:
+                on_vector = (3, 7)
+            else:
+                on_vector = (2, 4, 6)
             i = 0
-            for n in ((2, 2, 2, 2) if b == 0 else (4, 4)):
-                st = stage.tile([P, 2 * n, W], F32, name="st%d" % n, bufs={2: 4, 4: 8}[n])
+            for n in STORE_BANKS[b]:
+                staged = stage.tile([P, 2 * n, WIDTH], F32, name="staged%d" % n, bufs=STAGE_BUFS[n])
                 for s in range(n):
-                    acc = ps.tile([P, 2, W], F32, name="bank")
-                    for jj in range(2):
+                    acc = bank_pool.tile([P, 2, WIDTH], F32, name="bank")
+                    for j in range(2):
                         nc.tensor.matmul_mx(
-                            out=acc[:, jj, :],
-                            lhsT=l_q[i][0][:, P * jj:P * (jj + 1)].bitcast(FP8X4),
-                            lhsT_scale=l_q[i][1][:, P * jj:P * (jj + 1)],
-                            rhs=m_q[b][0][:].bitcast(FP8X4),
-                            rhs_scale=m_q[b][1][:],
+                            out=acc[:, j, :],
+                            lhsT=linc_mx[i][0][:, P * j:P * (j + 1)].bitcast(FP8X4),
+                            lhsT_scale=linc_mx[i][1][:, P * j:P * (j + 1)],
+                            rhs=m_mx[b][0][:].bitcast(FP8X4),
+                            rhs_scale=m_mx[b][1][:],
                             start=True,
                             stop=True,
                         )
                     if b == 0:
-                        if i + 6 < 8:
-                            transpose_l(i + 6)
-                        if i + 4 < 8:
-                            copy_l(i + 4)
-                        if i + 2 < 8:
-                            quantise_l(i + 2)
-                    elif i == 1 and b + 1 < B:
-                        messages(b + 1)
-                        quantise_m(b + 1)
-                    if b == 2 and i == 2:
-                        prepare_x(1)
-                    if b == 2 and i == 6:
-                        first_matmul(1)
-                    empty_bank(i in ((0, 4) if b == 0 else (2, 4, 6)), st[:, 2 * s:2 * s + 2, :], acc[:])
-                    if b == 0 and i == 3:
-                        messages(1)
-                        quantise_m(1)
+                        if i + AHEAD_TRANSPOSE < BANKS:
+                            transpose_linc(i + AHEAD_TRANSPOSE)
+                        if i + AHEAD_COPY < BANKS:
+                            copy_linc(i + AHEAD_COPY)
+                        if i + AHEAD_QUANTISE < BANKS:
+                            quantise_linc(i + AHEAD_QUANTISE)
+                    if new_group and i == 0:
+                        prepare_x(group_starts.index(b + 1))
+                    if new_group and i == 3:
+                        first_matmul(group_starts.index(b + 1))
+                    if b + 1 < SIGNALS and i == (5 if new_group else 1):
+                        quantise_messages(b + 1, messages(b + 1))
+                    empty_bank(i in on_vector, staged[:, 2 * s:2 * s + 2, :], acc[:])
                     i += 1
-                nc.sync.dma_start(out=o_view[b, :, 2 * (i - n):2 * i, :], in_=st[:])
+                nc.sync.dma_start(out=out_tiles[b, :, 2 * (i - n):2 * i, :], in_=staged[:])

@@ -17,10 +17,11 @@ NODE_PASSES = NODES // (P * PACK)
 EDGE_TILES = EDGES // P
 NODE_TILES = NODES // P
 BANKS = NODE_TILES // 2
+GROUP = P // CHANNELS
+PASS_WORDS = P * PACK // 2
+LOAD_TILES = 4
 
 FLOPS = 2 * EDGES * NODES * SIGNALS * CHANNELS + 2 * NODES * EDGES * SIGNALS * WIDTH
-
-X_GROUPS = ((0, 2), (2, 6), (6, 8))
 
 STORE_BANKS = ((1, 1, 2, 2, 2), (2, 2, 4)) + ((4, 4),) * 6
 STAGE_BUFS = {1: 2, 2: 5, 4: 8}
@@ -33,7 +34,7 @@ def tile_sgcn_pa_t_kernel(tc, x, rinc, linc, edge_w, out):
     with ExitStack() as ctx:
         keep = ctx.enter_context(tc.tile_pool(name="keep", bufs=1))
         stage = ctx.enter_context(tc.tile_pool(name="stage", bufs=1))
-        z_pool = ctx.enter_context(tc.psum_pool(name="z_pool", bufs=2))
+        z_pool = ctx.enter_context(tc.psum_pool(name="z_pool", bufs=SIGNALS // GROUP))
         bank_pool = ctx.enter_context(tc.psum_pool(name="bank_pool", bufs=6))
         ctx.enter_context(tc.manual_schedule())
 
@@ -43,34 +44,27 @@ def tile_sgcn_pa_t_kernel(tc, x, rinc, linc, edge_w, out):
         edge_w_rows = keep.tile([P, 2, 2 * KERNELS], BF16, name="edge_w_rows")
         nc.scalar.dma_start(out=edge_w_rows[:], in_=edge_w.rearrange("(u p e) k -> p u (e k)", u=2, p=P, e=2))
 
-        x_rows = [keep.tile([P, hi - lo, NODE_PASSES, PACK * CHANNELS], BF16, name="x_rows%d" % lo) for lo, hi in X_GROUPS]
-        x_grouped = [
-            keep.tile([P, NODE_PASSES, P * PACK], BF16, name="x_grouped%d" % lo, align_bytes=64) for lo, hi in X_GROUPS
-        ]
+        x_rows = [keep.tile([P, GROUP, NODE_PASSES, PACK * CHANNELS], BF16, name="x_rows%d" % h) for h in range(2)]
         rinc_rows = [keep.tile([P, NODES], BF16, name="rinc_rows%d" % t) for t in range(EDGE_TILES - 1)]
         rinc_last = [keep.tile([P, NODES // 2], BF16, name="rinc_last%d" % half) for half in range(2)]
-        linc_rows = [keep.tile([P, 4, EDGES], BF16, name="linc_rows%d" % q) for q in range(NODE_TILES // 4)]
+        linc_rows = [keep.tile([P, LOAD_TILES, EDGES], BF16, name="linc_rows%d" % q) for q in range(NODE_TILES // LOAD_TILES)]
         rinc_tiles = rinc.rearrange("(u p e) n -> u e p n", u=2, p=P, e=2)
         linc_tiles = linc.rearrange("(p j) e -> p j e", j=NODE_TILES)
 
         def load_x(h):
-            lo, hi = X_GROUPS[h]
-            if hi - lo < 4:
-                nc.gpsimd.memset(x_grouped[h][:], 0.0)
             nc.sync.dma_start(
                 out=x_rows[h][:],
-                in_=x[lo:hi].rearrange("b (g p t) c -> p b g (t c)", g=NODE_PASSES, p=P, t=PACK),
+                in_=x[GROUP * h:GROUP * (h + 1)].rearrange("b (g p t) c -> p b g (t c)", g=NODE_PASSES, p=P, t=PACK),
             )
 
         load_x(0)
         for t in range(EDGE_TILES - 1):
             nc.sync.dma_start(out=rinc_rows[t][:], in_=rinc_tiles[t // 2, t % 2])
         for half in range(2):
-            nc.sync.dma_start(out=rinc_last[half][:], in_=rinc_tiles[1, 1][:, 1024 * half:1024 * (half + 1)])
-        for q in range(NODE_TILES // 4):
-            nc.sync.dma_start(out=linc_rows[q][:], in_=linc_tiles[:, 4 * q:4 * q + 4, :])
+            nc.sync.dma_start(out=rinc_last[half][:], in_=rinc_tiles[1, 1][:, NODES // 2 * half:NODES // 2 * (half + 1)])
+        for q in range(NODE_TILES // LOAD_TILES):
+            nc.sync.dma_start(out=linc_rows[q][:], in_=linc_tiles[:, LOAD_TILES * q:LOAD_TILES * (q + 1), :])
         load_x(1)
-        load_x(2)
 
         edge_w_f32 = keep.tile([P, KERNELS, PACK], F32, name="edge_w_f32")
         nc.vector.tensor_copy(
@@ -90,17 +84,16 @@ def tile_sgcn_pa_t_kernel(tc, x, rinc, linc, edge_w, out):
             nc.vector.quantize_mx(out=codes[:].bitcast(FP8X4), scales=scales[:], in_=grouped)
             return codes, scales
 
-        x_mx = [None] * len(X_GROUPS)
+        x_mx = [None, None]
 
         def prepare_x(h):
-            lo, hi = X_GROUPS[h]
+            grouped = keep.tile([P, NODE_PASSES, P * PACK], BF16, name="x_grouped%d" % h, align_bytes=64)
             for g in range(NODE_PASSES):
-                filled = x_grouped[h][:, g, 0:(hi - lo) * CHANNELS * PACK]
                 nc.vector.tensor_copy(
-                    out=filled.rearrange("p (b c t) -> p b c t", b=hi - lo, c=CHANNELS),
+                    out=grouped[:, g, :].rearrange("p (b c t) -> p b c t", b=GROUP, c=CHANNELS),
                     in_=x_rows[h][:, :, g, :].rearrange("p b (t c) -> p b c t", t=PACK),
                 )
-            x_mx[h] = quantise("x%d" % h, x_grouped[h][:].rearrange("p g w -> p (g w)"), NODE_PASSES * P * PACK)
+            x_mx[h] = quantise("x%d" % h, grouped[:].rearrange("p g w -> p (g w)"), NODE_PASSES * P * PACK)
 
         prepare_x(0)
 
@@ -112,23 +105,26 @@ def tile_sgcn_pa_t_kernel(tc, x, rinc, linc, edge_w, out):
 
         for i in range(2 * EDGE_TILES):
             t, half = i // 2, i % 2
-            rows = rinc_rows[t][:, 1024 * half:1024 * (half + 1)] if t < EDGE_TILES - 1 else rinc_last[half][:]
+            if t < EDGE_TILES - 1:
+                rows = rinc_rows[t][:, NODES // 2 * half:NODES // 2 * (half + 1)]
+            else:
+                rows = rinc_last[half][:]
             words = rows.bitcast(F32)
             bank = bank_pool.tile([P, 2, 2, P], F32, name="bank")
-            for g in range(2):
+            for s in range(2):
                 for pair in range(2):
-                    nc.tensor.transpose(bank[:, g, pair, :], words[:, 256 * g + pair:256 * (g + 1):2], identity[:])
+                    nc.tensor.transpose(bank[:, s, pair, :], words[:, PASS_WORDS * s + pair:PASS_WORDS * (s + 1):2], identity[:])
             rinc_grouped[i] = keep.tile([P, 2 * P * PACK], BF16, name="rinc_grouped%d" % i, align_bytes=64)
             empty_bank(
                 i % 4 == 1,
-                rinc_grouped[i][:].bitcast(F32).rearrange("p (g e pair) -> p g e pair", g=2, pair=2),
-                bank[:].rearrange("p g pair e -> p g e pair"),
+                rinc_grouped[i][:].bitcast(F32).rearrange("p (s e pair) -> p s e pair", s=2, pair=2),
+                bank[:].rearrange("p s pair e -> p s e pair"),
             )
             if i >= 1:
                 quantise_rinc(i - 1)
         quantise_rinc(2 * EDGE_TILES - 1)
 
-        z = [None] * len(X_GROUPS)
+        z = [None, None]
 
         def first_matmul(h):
             z[h] = z_pool.tile([P, EDGE_TILES, P], F32, name="z")
@@ -151,18 +147,19 @@ def tile_sgcn_pa_t_kernel(tc, x, rinc, linc, edge_w, out):
         linc_mx = [None] * BANKS
 
         def transpose_linc(i):
-            words = linc_rows[i // 2][:].bitcast(F32)
             linc_bank[i] = bank_pool.tile([P, 2, 2, P], F32, name="bank")
-            for j in range(2):
+            for s in range(2):
+                j = 2 * i + s
+                words = linc_rows[j // LOAD_TILES][:, j % LOAD_TILES, :].bitcast(F32)
                 for u in range(2):
-                    nc.tensor.transpose(linc_bank[i][:, j, u, :], words[:, 2 * (i % 2) + j, P * u:P * (u + 1)], identity[:])
+                    nc.tensor.transpose(linc_bank[i][:, s, u, :], words[:, P * u:P * (u + 1)], identity[:])
 
         def copy_linc(i):
             linc_grouped[i] = keep.tile([P, 2 * P * PACK], BF16, name="linc_grouped%d" % i, align_bytes=64)
             empty_bank(
                 i == BANKS - 1,
-                linc_grouped[i][:].bitcast(F32).rearrange("p (j n u) -> p j n u", j=2, u=2),
-                linc_bank[i][:].rearrange("p j u n -> p j n u"),
+                linc_grouped[i][:].bitcast(F32).rearrange("p (s n u) -> p s n u", s=2, u=2),
+                linc_bank[i][:].rearrange("p s u n -> p s n u"),
             )
 
         def quantise_linc(i):
@@ -171,13 +168,12 @@ def tile_sgcn_pa_t_kernel(tc, x, rinc, linc, edge_w, out):
         m_mx = [None] * SIGNALS
 
         def messages(b):
-            h = [lo <= b < hi for lo, hi in X_GROUPS].index(True)
-            first = CHANNELS * (b - X_GROUPS[h][0])
+            first = CHANNELS * (b % GROUP)
             shape = [P, CHANNELS, KERNELS, PACK]
             grouped = keep.tile([P, WIDTH * PACK], BF16, name="m_grouped%d" % b, align_bytes=64)
             nc.vector.tensor_tensor(
                 out=grouped[:].rearrange("p (c k t) -> p c k t", c=CHANNELS, k=KERNELS),
-                in0=z[h][:, :, first:first + CHANNELS].rearrange("p t c -> p c t").unsqueeze(2).to_broadcast(shape),
+                in0=z[b // GROUP][:, :, first:first + CHANNELS].rearrange("p t c -> p c t").unsqueeze(2).to_broadcast(shape),
                 in1=edge_w_f32[:].unsqueeze(1).to_broadcast(shape),
                 op=mybir.AluOpType.mult,
             )
@@ -199,9 +195,8 @@ def tile_sgcn_pa_t_kernel(tc, x, rinc, linc, edge_w, out):
             quantise_linc(i)
 
         out_tiles = out.rearrange("b (p j) w -> b p j w", j=NODE_TILES)
-        group_starts = [lo for lo, hi in X_GROUPS]
         for b in range(SIGNALS):
-            new_group = b + 1 in group_starts
+            new_group = b + 1 == GROUP
             if b == 0:
                 on_vector = ()
             elif new_group:
@@ -211,13 +206,13 @@ def tile_sgcn_pa_t_kernel(tc, x, rinc, linc, edge_w, out):
             i = 0
             for n in STORE_BANKS[b]:
                 staged = stage.tile([P, 2 * n, WIDTH], F32, name="staged%d" % n, bufs=STAGE_BUFS[n])
-                for s in range(n):
+                for slot in range(n):
                     acc = bank_pool.tile([P, 2, WIDTH], F32, name="bank")
-                    for j in range(2):
+                    for s in range(2):
                         nc.tensor.matmul_mx(
-                            out=acc[:, j, :],
-                            lhsT=linc_mx[i][0][:, P * j:P * (j + 1)].bitcast(FP8X4),
-                            lhsT_scale=linc_mx[i][1][:, P * j:P * (j + 1)],
+                            out=acc[:, s, :],
+                            lhsT=linc_mx[i][0][:, P * s:P * (s + 1)].bitcast(FP8X4),
+                            lhsT_scale=linc_mx[i][1][:, P * s:P * (s + 1)],
                             rhs=m_mx[b][0][:].bitcast(FP8X4),
                             rhs_scale=m_mx[b][1][:],
                             start=True,
@@ -231,11 +226,11 @@ def tile_sgcn_pa_t_kernel(tc, x, rinc, linc, edge_w, out):
                         if i + AHEAD_QUANTISE < BANKS:
                             quantise_linc(i + AHEAD_QUANTISE)
                     if new_group and i == 0:
-                        prepare_x(group_starts.index(b + 1))
+                        prepare_x(1)
                     if new_group and i == 3:
-                        first_matmul(group_starts.index(b + 1))
+                        first_matmul(1)
                     if b + 1 < SIGNALS and i == (5 if new_group else 1):
                         quantise_messages(b + 1, messages(b + 1))
-                    empty_bank(i in on_vector, staged[:, 2 * s:2 * s + 2, :], acc[:])
+                    empty_bank(i in on_vector, staged[:, 2 * slot:2 * slot + 2, :], acc[:])
                     i += 1
                 nc.sync.dma_start(out=out_tiles[b, :, 2 * (i - n):2 * i, :], in_=staged[:])

@@ -36,7 +36,6 @@ def tile_sgcn_pa_t_kernel(tc, x, rinc, linc, edge_w, out):
         stage = ctx.enter_context(tc.tile_pool(name="stage", bufs=1))
         z_pool = ctx.enter_context(tc.psum_pool(name="z_pool", bufs=SIGNALS // GROUP))
         bank_pool = ctx.enter_context(tc.psum_pool(name="bank_pool", bufs=6))
-        ctx.enter_context(tc.manual_schedule())
 
         identity = keep.tile([P, P], F32, name="identity")
         make_identity(nc, identity[:])

from contextlib import ExitStack

import concourse.mybir as mybir
from concourse.masks import make_identity

FP8X4 = mybir.dt.float8_e4m3fn_x4
BF16 = mybir.dt.bfloat16
F32 = mybir.dt.float32
U32 = mybir.dt.uint32
U8 = mybir.dt.uint8

P = 128
PACK = 4
SIGNALS, NODES, EDGES, CHANNELS, KERNELS = 8, 2048, 512, 32, 8
WIDTH = CHANNELS * KERNELS
NODE_PASSES = NODES // (P * PACK)
EDGE_TILES = EDGES // P
NODE_TILES = NODES // P
BANKS = NODE_TILES // 2
GROUP = P // CHANNELS
PASS_WORDS = P * PACK // 2
LOAD_TILES = 4

FLOPS = 2 * EDGES * NODES * SIGNALS * CHANNELS + 2 * NODES * EDGES * SIGNALS * WIDTH

STORE_BANKS = ((1, 1, 2, 2, 2), (2, 2, 4)) + ((4, 4),) * 6
STAGE_BUFS = {1: 2, 2: 5, 4: 8}

AHEAD_TRANSPOSE, AHEAD_COPY, AHEAD_QUANTISE = 6, 5, 2


def tile_sgcn_pa_t_kernel(tc, x, rinc, linc, edge_w, out):
    nc = tc.nc
    with ExitStack() as ctx:
        keep = ctx.enter_context(tc.tile_pool(name="keep", bufs=1))
        stage = ctx.enter_context(tc.tile_pool(name="stage", bufs=1))
        z_pool = ctx.enter_context(tc.psum_pool(name="z_pool", bufs=SIGNALS // GROUP))
        bank_pool = ctx.enter_context(tc.psum_pool(name="bank_pool", bufs=6))

        identity = keep.tile([P, P], F32, name="identity")
        make_identity(nc, identity[:])

        edge_w_rows = keep.tile([P, 2, 2 * KERNELS], BF16, name="edge_w_rows")
        nc.scalar.dma_start(out=edge_w_rows[:], in_=edge_w.rearrange("(u p e) k -> p u (e k)", u=2, p=P, e=2))

        x_rows = [keep.tile([P, GROUP, NODE_PASSES, PACK * CHANNELS], BF16, name="x_rows%d" % h) for h in range(2)]
        rinc_rows = [keep.tile([P, NODES], BF16, name="rinc_rows%d" % t) for t in range(EDGE_TILES - 1)]
        rinc_last = [keep.tile([P, NODES // 2], BF16, name="rinc_last%d" % half) for half in range(2)]
        linc_rows = [keep.tile([P, LOAD_TILES, EDGES], BF16, name="linc_rows%d" % q) for q in range(NODE_TILES // LOAD_TILES)]
        rinc_tiles = rinc.rearrange("(u p e) n -> u e p n", u=2, p=P, e=2)
        linc_tiles = linc.rearrange("(p j) e -> p j e", j=NODE_TILES)

        def load_x(h):
            nc.sync.dma_start(
                out=x_rows[h][:],
                in_=x[GROUP * h:GROUP * (h + 1)].rearrange("b (g p t) c -> p b g (t c)", g=NODE_PASSES, p=P, t=PACK),
            )

        load_x(0)
        for t in range(EDGE_TILES - 1):
            nc.sync.dma_start(out=rinc_rows[t][:], in_=rinc_tiles[t // 2, t % 2])
        for half in range(2):
            nc.sync.dma_start(out=rinc_last[half][:], in_=rinc_tiles[1, 1][:, NODES // 2 * half:NODES // 2 * (half + 1)])
        for q in range(NODE_TILES // LOAD_TILES):
            nc.sync.dma_start(out=linc_rows[q][:], in_=linc_tiles[:, LOAD_TILES * q:LOAD_TILES * (q + 1), :])
        load_x(1)

        edge_w_f32 = keep.tile([P, KERNELS, PACK], F32, name="edge_w_f32")
        nc.vector.tensor_copy(
            out=edge_w_f32[:].rearrange("p k (u e) -> p k u e", u=2),
            in_=edge_w_rows[:].rearrange("p u (e k) -> p k u e", e=2),
        )

        def empty_bank(on_vector, dst, src):
            if on_vector:
                nc.vector.tensor_copy(out=dst, in_=src)
            else:
                nc.scalar.copy(out=dst, in_=src)

        def quantise(name, grouped, width):
            codes = keep.tile([P, width // PACK], U32, name="codes_" + name, align_bytes=64)
            scales = keep.tile([P, width // PACK], U8, name="scales_" + name, align_bytes=64)
            nc.vector.quantize_mx(out=codes[:].bitcast(FP8X4), scales=scales[:], in_=grouped)
            return codes, scales

        x_mx = [None, None]

        def prepare_x(h):
            grouped = keep.tile([P, NODE_PASSES, P * PACK], BF16, name="x_grouped%d" % h, align_bytes=64)
            for g in range(NODE_PASSES):
                nc.vector.tensor_copy(
                    out=grouped[:, g, :].rearrange("p (b c t) -> p b c t", b=GROUP, c=CHANNELS),
                    in_=x_rows[h][:, :, g, :].rearrange("p b (t c) -> p b c t", t=PACK),
                )
            x_mx[h] = quantise("x%d" % h, grouped[:].rearrange("p g w -> p (g w)"), NODE_PASSES * P * PACK)

        prepare_x(0)

        rinc_grouped = [None] * (2 * EDGE_TILES)
        rinc_mx = [None] * (2 * EDGE_TILES)

        def quantise_rinc(i):
            rinc_mx[i] = quantise("rinc%d" % i, rinc_grouped[i][:], 2 * P * PACK)

        for i in range(2 * EDGE_TILES):
            t, half = i // 2, i % 2
            if t < EDGE_TILES - 1:
                rows = rinc_rows[t][:, NODES // 2 * half:NODES // 2 * (half + 1)]
            else:
                rows = rinc_last[half][:]
            words = rows.bitcast(F32)
            bank = bank_pool.tile([P, 2, 2, P], F32, name="bank")
            for s in range(2):
                for pair in range(2):
                    nc.tensor.transpose(bank[:, s, pair, :], words[:, PASS_WORDS * s + pair:PASS_WORDS * (s + 1):2], identity[:])
            rinc_grouped[i] = keep.tile([P, 2 * P * PACK], BF16, name="rinc_grouped%d" % i, align_bytes=64)
            empty_bank(
                i % 4 == 1,
                rinc_grouped[i][:].bitcast(F32).rearrange("p (s e pair) -> p s e pair", s=2, pair=2),
                bank[:].rearrange("p s pair e -> p s e pair"),
            )
            if i >= 1:
                quantise_rinc(i - 1)
        quantise_rinc(2 * EDGE_TILES - 1)

        z = [None, None]

        def first_matmul(h):
            z[h] = z_pool.tile([P, EDGE_TILES, P], F32, name="z")
            for t in range(EDGE_TILES):
                for g in range(NODE_PASSES):
                    codes, scales = rinc_mx[2 * t + g // 2]
                    edges = slice(P * (g % 2), P * (g % 2 + 1))
                    nc.tensor.matmul_mx(
                        out=z[h][:, t, :],
                        lhsT=codes[:, edges].bitcast(FP8X4),
                        lhsT_scale=scales[:, edges],
                        rhs=x_mx[h][0][:, P * g:P * (g + 1)].bitcast(FP8X4),
                        rhs_scale=x_mx[h][1][:, P * g:P * (g + 1)],
                        start=(g == 0),
                        stop=(g == NODE_PASSES - 1),
                    )

        linc_bank = [None] * BANKS
        linc_grouped = [None] * BANKS
        linc_mx = [None] * BANKS

        def transpose_linc(i):
            linc_bank[i] = bank_pool.tile([P, 2, 2, P], F32, name="bank")
            for s in range(2):
                j = 2 * i + s
                words = linc_rows[j // LOAD_TILES][:, j % LOAD_TILES, :].bitcast(F32)
                for u in range(2):
                    nc.tensor.transpose(linc_bank[i][:, s, u, :], words[:, P * u:P * (u + 1)], identity[:])

        def copy_linc(i):
            linc_grouped[i] = keep.tile([P, 2 * P * PACK], BF16, name="linc_grouped%d" % i, align_bytes=64)
            empty_bank(
                i == BANKS - 1,
                linc_grouped[i][:].bitcast(F32).rearrange("p (s n u) -> p s n u", s=2, u=2),
                linc_bank[i][:].rearrange("p s u n -> p s n u"),
            )

        def quantise_linc(i):
            linc_mx[i] = quantise("linc%d" % i, linc_grouped[i][:], 2 * P * PACK)

        m_mx = [None] * SIGNALS

        def messages(b):
            first = CHANNELS * (b % GROUP)
            shape = [P, CHANNELS, KERNELS, PACK]
            grouped = keep.tile([P, WIDTH * PACK], BF16, name="m_grouped%d" % b, align_bytes=64)
            nc.vector.tensor_tensor(
                out=grouped[:].rearrange("p (c k t) -> p c k t", c=CHANNELS, k=KERNELS),
                in0=z[b // GROUP][:, :, first:first + CHANNELS].rearrange("p t c -> p c t").unsqueeze(2).to_broadcast(shape),
                in1=edge_w_f32[:].unsqueeze(1).to_broadcast(shape),
                op=mybir.AluOpType.mult,
            )
            return grouped

        def quantise_messages(b, grouped):
            m_mx[b] = quantise("m%d" % b, grouped[:], WIDTH * PACK)

        transpose_linc(0)
        first_matmul(0)
        for i in range(1, AHEAD_TRANSPOSE):
            transpose_linc(i)
        for i in range(AHEAD_COPY):
            copy_linc(i)
        m_grouped = messages(0)
        quantise_linc(0)
        quantise_messages(0, m_grouped)
        for i in range(1, AHEAD_QUANTISE):
            quantise_linc(i)

        out_tiles = out.rearrange("b (p j) w -> b p j w", j=NODE_TILES)
        for b in range(SIGNALS):
            new_group = b + 1 == GROUP
            if b == 0:
                on_vector = ()
            elif new_group:
                on_vector = (3, 7)
            else:
                on_vector = (2, 4, 6)
            i = 0
            for n in STORE_BANKS[b]:
                staged = stage.tile([P, 2 * n, WIDTH], F32, name="staged%d" % n, bufs=STAGE_BUFS[n])
                for slot in range(n):
                    acc = bank_pool.tile([P, 2, WIDTH], F32, name="bank")
                    for s in range(2):
                        nc.tensor.matmul_mx(
                            out=acc[:, s, :],
                            lhsT=linc_mx[i][0][:, P * s:P * (s + 1)].bitcast(FP8X4),
                            lhsT_scale=linc_mx[i][1][:, P * s:P * (s + 1)],
                            rhs=m_mx[b][0][:].bitcast(FP8X4),
                            rhs_scale=m_mx[b][1][:],
                            start=True,
                            stop=True,
                        )
                    if b == 0:
                        if i + AHEAD_TRANSPOSE < BANKS:
                            transpose_linc(i + AHEAD_TRANSPOSE)
                        if i + AHEAD_COPY < BANKS:
                            copy_linc(i + AHEAD_COPY)
                        if i + AHEAD_QUANTISE < BANKS:
                            quantise_linc(i + AHEAD_QUANTISE)
                    if new_group and i == 0:
                        prepare_x(1)
                    if new_group and i == 3:
                        first_matmul(1)
                    if b + 1 < SIGNALS and i == (5 if new_group else 1):
                        quantise_messages(b + 1, messages(b + 1))
                    empty_bank(i in on_vector, staged[:, 2 * slot:2 * slot + 2, :], acc[:])
                    i += 1
                nc.sync.dma_start(out=out_tiles[b, :, 2 * (i - n):2 * i, :], in_=staged[:])
